import numpy as np
import ml_dtypes


def mxq(x, axis, fmt="e4m3"):
    dtype, down = {"e4m3": (ml_dtypes.float8_e4m3fn, 7), "e5m2": (ml_dtypes.float8_e5m2, 14)}[fmt]
    v = np.moveaxis(np.asarray(x, np.float32).astype(ml_dtypes.bfloat16).astype(np.float64), axis, -1)
    blocks = v.reshape(v.shape[:-1] + (-1, 32))
    amax = np.abs(blocks).max(-1, keepdims=True)
    byte = np.maximum(np.where(amax > 0, np.frexp(amax)[1] - 1 + 127, 0) - down, 1)
    scale = np.exp2(byte - 127.0)
    codes = (blocks / scale).astype(np.float32).astype(dtype).astype(np.float64)
    return np.moveaxis((codes * scale).reshape(v.shape), -1, axis)


WIDE = False


def mx_kscale(k):
    if not WIDE:
        return np.ones(k)
    levels = np.array([10, -10, 5, -5, 0])
    a = np.random.permutation(np.resize(levels, k // 512 * 4)).reshape(k // 512, 4)
    idx = np.arange(k)
    return np.exp2(a[idx // 512, idx % 128 // 32])


BF16 = ml_dtypes.bfloat16


def bf(x):
    return np.asarray(x, np.float32).astype(BF16)


def f64(x):
    return np.asarray(x).astype(np.float64)


E2M1 = np.array([0.0, 0.5, 1.0, 1.5, 2.0, 3.0, 4.0, 6.0, -0.0, -0.5, -1.0, -1.5, -2.0, -3.0, -4.0, -6.0])


def pack_weight(w, fmt):
    k, n = w.shape
    w = f64(bf(w)).reshape(k // 32, 32, n)
    amax = np.abs(w).max(1)
    if fmt == "e4m3":
        byte = np.frexp(amax)[1] - 1 + 127 - 7
    else:
        mant, ex = np.frexp(amax / 6.0)
        byte = np.where(mant > 0.5, ex, ex - 1) + 127
    byte = np.clip(np.where(amax > 0, byte, 1), 1, 254)
    scaled = (w * np.exp2(127.0 - byte)[:, None, :]).reshape(k, n).astype(np.float32)
    by_word = np.ascontiguousarray(scaled.reshape(k // 512, 128, 4, n).transpose(0, 1, 3, 2))
    if fmt == "e4m3":
        words = by_word.astype(ml_dtypes.float8_e4m3fn).view(np.uint8)
    else:
        c = by_word.astype(ml_dtypes.float4_e2m1fn).view(np.uint8) & 0xF
        words = c[..., 0::2] | (c[..., 1::2] << 4)
    return np.ascontiguousarray(words), np.ascontiguousarray(byte.astype(np.uint8).reshape(k // 512, 16, n))


def unpack_weight(words, scales, fmt):
    g, p, n, _ = words.shape
    if fmt == "e4m3":
        vals = np.ascontiguousarray(words).view(ml_dtypes.float8_e4m3fn).astype(np.float64)
    else:
        nib = np.empty((g, p, n, 4), np.uint8)
        nib[..., 0::2] = words & 0xF
        nib[..., 1::2] = words >> 4
        vals = E2M1[nib]
    vals = vals * np.repeat(np.exp2(scales.astype(np.float64) - 127.0), 8, axis=1)[..., None]
    return vals.transpose(0, 1, 3, 2).reshape(g * 512, n)


B, H, W, C, HIDDEN = 4, 16, 16, 512, 2048
FMT = "e4m3"


def _perceive(x):
    r = lambda di, dj: np.roll(x, shift=(-di, -dj), axis=(1, 2))
    sx = (r(-1, 1) - r(-1, -1)) + 2.0 * (r(0, 1) - r(0, -1)) + (r(1, 1) - r(1, -1))
    sy = (r(1, -1) - r(-1, -1)) + 2.0 * (r(1, 0) - r(-1, 0)) + (r(1, 1) - r(-1, 1))
    return np.concatenate([sx, sy, x], axis=-1)


def setup_inputs():
    s = mx_kscale(C)
    s3 = np.tile(s, 3)
    t = mx_kscale(HIDDEN)
    state_grid = bf(np.random.standard_normal((B, H, W, C)) * s)
    w_hidden = np.random.standard_normal((HIDDEN, 3 * C)) * 0.6 / np.sqrt(3 * C) / s3[None, :] * t[:, None]
    w_out = np.random.standard_normal((C, HIDDEN)) / np.sqrt(HIDDEN) / t[None, :]
    wh_words, wh_scales = pack_weight(np.ascontiguousarray(w_hidden.T), FMT)
    wo_words, wo_scales = pack_weight(np.ascontiguousarray(w_out.T), FMT)
    return {"state_grid": state_grid,
            "W_hidden_words": wh_words, "W_hidden_scales": wh_scales,
            "W_out_words": wo_words, "W_out_scales": wo_scales}


def reference(state_grid, W_hidden_words, W_hidden_scales, W_out_words, W_out_scales):
    perception = _perceive(f64(state_grid))
    hidden = np.maximum(mxq(perception, 3, "e4m3") @ unpack_weight(W_hidden_words, W_hidden_scales, FMT), 0.0)
    delta_s = mxq(hidden, 3, "e4m3") @ unpack_weight(W_out_words, W_out_scales, FMT)
    return delta_s

@@ -1,0 +1,243 @@
+from contextlib import ExitStack
+
+import concourse.mybir as mybir
+from concourse.masks import make_identity
+
+F32 = mybir.dt.float32
+BF16 = mybir.dt.bfloat16
+I32 = mybir.dt.int32
+U32 = mybir.dt.uint32
+U8 = mybir.dt.uint8
+FP8X4 = mybir.dt.float8_e4m3fn_x4
+ALU = mybir.AluOpType
+RELU = mybir.ActivationFunctionType.Relu
+
+P = 128
+PACK = 4
+K_PASS = P * PACK
+BANK = 512
+
+IMAGES, SIDE, CHANNELS, HIDDEN = 4, 16, 512, 2048
+HALVES = SIDE * SIDE // P
+PIXEL_TILES = IMAGES * HALVES
+FILTERS = 3
+HIDDEN_PASSES = HIDDEN // K_PASS
+PAIR = 2
+PADDED = SIDE + 2
+
+LEAD = 2
+
+FLOPS = 2 * IMAGES * SIDE * SIDE * (FILTERS * CHANNELS * HIDDEN + HIDDEN * CHANNELS)
+
+
+def tile_nn_kernel(tc, state_grid, w_hidden_words, w_hidden_scales, w_out_words, w_out_scales, out):
+    nc = tc.nc
+    state_rows = state_grid.rearrange("b h w c -> (b h w) c")
+    out_rows = out.rearrange("b h w c -> (b h w) c")
+
+    with ExitStack() as stack:
+        stack.enter_context(tc.manual_schedule())
+        keep = stack.enter_context(tc.tile_pool(name="keep", bufs=1))
+        work = stack.enter_context(tc.tile_pool(name="work", bufs=2))
+        psum = stack.enter_context(tc.psum_pool(name="psum", bufs=8))
+
+        wh_planes = keep.tile([P, HIDDEN], U8, align_bytes=64)
+        wo_planes = keep.tile([P, CHANNELS], U8, align_bytes=64)
+        nc.vector.memset(wh_planes[:].bitcast(I32), 0)
+        nc.vector.memset(wo_planes[:].bitcast(I32), 0)
+
+        def load_image(b):
+            raw = keep.tile([P, HALVES, CHANNELS], BF16, name="state%d" % b)
+            rows = state_rows[b * HALVES * P : (b + 1) * HALVES * P, :]
+            nc.sync.dma_start(out=raw[:], in_=rows.rearrange("(half q) c -> q half c", q=P))
+            return raw
+
+        def load_planes(planes, scales):
+            passes = scales.shape[0]
+            for quadrant in range(4):
+                nc.sync.dma_start(
+                    out=planes[32 * quadrant : 32 * quadrant + 4 * passes, :].bitcast(I32),
+                    in_=scales[:, 4 * quadrant : 4 * quadrant + 4, :].bitcast(I32),
+                )
+
+        state = [load_image(b) for b in range(2)]
+        load_planes(wh_planes, w_hidden_scales)
+        wh_bytes = w_hidden_words.rearrange("f p n t -> p f (n t)")
+        wh_words = []
+        for g in range(HIDDEN_PASSES):
+            block = keep.tile([P, FILTERS, BANK], U32, name="wh_words%d" % g, align_bytes=64)
+            nc.sync.dma_start(
+                out=block[:].bitcast(I32),
+                in_=wh_bytes[:, :, g * BANK * PACK : (g + 1) * BANK * PACK].bitcast(I32),
+            )
+            wh_words.append(block)
+        state.extend([load_image(b) for b in range(2, IMAGES)])
+        load_planes(wo_planes, w_out_scales)
+        wo_words = keep.tile([P, HIDDEN_PASSES, CHANNELS], U32, align_bytes=64)
+        nc.sync.dma_start(
+            out=wo_words[:].bitcast(I32),
+            in_=w_out_words.rearrange("g p n t -> p g (n t)").bitcast(I32),
+        )
+
+        ident_bf16 = keep.tile([P, P], BF16)
+        make_identity(nc, ident_bf16[:])
+        ident_f32 = keep.tile([P, P], F32)
+        make_identity(nc, ident_f32[:])
+
+        shifted = keep.tile([P, PADDED, PADDED], BF16)
+        nc.vector.memset(shifted[:], 0.0)
+        nc.vector.tensor_copy(
+            out=shifted[:, 1 : 1 + SIDE // HALVES, 1 : 1 + SIDE],
+            in_=ident_bf16[:].rearrange("k (i j) -> k i j", j=SIDE),
+        )
+        nc.vector.tensor_copy(out=shifted[:, SIDE + 1 :, 1 : 1 + SIDE], in_=shifted[:, 1:2, 1 : 1 + SIDE])
+        nc.vector.tensor_copy(out=shifted[:, :, 0:1], in_=shifted[:, :, SIDE : SIDE + 1])
+        nc.vector.tensor_copy(out=shifted[:, :, SIDE + 1 :], in_=shifted[:, :, 1:2])
+
+        taps = keep.tile([P, FILTERS, HALVES * P], BF16)
+        diff_x = keep.tile([P, PADDED, SIDE], BF16)
+        nc.vector.tensor_sub(out=diff_x[:], in0=shifted[:, :, 2:], in1=shifted[:, :, :SIDE])
+        part_x = keep.tile([P, SIDE, SIDE], BF16)
+        nc.vector.scalar_tensor_tensor(
+            out=part_x[:], in0=diff_x[:, 1 : 1 + SIDE, :], scalar=2.0, in1=diff_x[:, :SIDE, :], op0=ALU.mult, op1=ALU.add
+        )
+        nc.vector.tensor_add(
+            out=taps[:, 0, :].rearrange("k (i j) -> k i j", j=SIDE), in0=part_x[:], in1=diff_x[:, 2:, :]
+        )
+        diff_y = keep.tile([P, SIDE, PADDED], BF16)
+        nc.vector.tensor_sub(out=diff_y[:], in0=shifted[:, 2:, :], in1=shifted[:, :SIDE, :])
+        part_y = keep.tile([P, SIDE, SIDE], BF16)
+        nc.vector.scalar_tensor_tensor(
+            out=part_y[:], in0=diff_y[:, :, 1 : 1 + SIDE], scalar=2.0, in1=diff_y[:, :, :SIDE], op0=ALU.mult, op1=ALU.add
+        )
+        nc.vector.tensor_add(
+            out=taps[:, 1, :].rearrange("k (i j) -> k i j", j=SIDE), in0=part_y[:], in1=diff_y[:, :, 2:]
+        )
+        nc.vector.tensor_copy(out=taps[:, 2, :P], in_=ident_bf16[:])
+
+        sorted_state = {}
+        grouped_perception = {}
+        perception_words = {}
+        perception_scales = {}
+        hidden_rows = {}
+        hidden_words = {}
+        hidden_scales = {}
+
+        def sort_channels(b):
+            by_t = keep.tile([P, HALVES, PACK, P], BF16, name="sorted%d" % b)
+            nc.scalar.copy(out=by_t[:], in_=state[b][:].rearrange("q half (p t) -> q half t p", t=PACK))
+            sorted_state[b] = by_t
+
+        def filter_tile(tile_no):
+            b, half = divmod(tile_no, HALVES)
+            perception = work.tile([P, FILTERS, P, PACK], BF16, align_bytes=64)
+            for f in range(FILTERS):
+                sources = (half,) if f == FILTERS - 1 else tuple(range(HALVES))
+                bank = psum.tile([P, PACK, P], F32, tag="bank")
+                for t in range(PACK):
+                    for source in sources:
+                        own_or_other = (half - source) % HALVES
+                        nc.tensor.matmul(
+                            out=bank[:, t, :],
+                            lhsT=sorted_state[b][:, source, t, :],
+                            rhs=taps[:, f, own_or_other * P : (own_or_other + 1) * P],
+                            start=(source == sources[0]),
+                            stop=(source == sources[-1]),
+                        )
+                nc.vector.tensor_copy(out=perception[:, f], in_=bank[:].rearrange("p t q -> p q t"))
+            grouped_perception[tile_no] = perception
+
+        def quantise_perception(tile_no):
+            words = keep.tile([P, FILTERS, P], U32, name="perception_words%d" % tile_no, align_bytes=64)
+            scales = keep.tile([P, FILTERS, P], U8, name="perception_scales%d" % tile_no, align_bytes=64)
+            for f in range(FILTERS):
+                nc.vector.quantize_mx(
+                    out=words[:, f, :].bitcast(FP8X4),
+                    scales=scales[:, f, :],
+                    in_=grouped_perception[tile_no][:, f].rearrange("p q t -> p (q t)"),
+                )
+            perception_words[tile_no] = words
+            perception_scales[tile_no] = scales
+
+        def first_layer(tile_no):
+            rows = work.tile([P, HIDDEN_PASSES, PAIR, P * PAIR], BF16)
+            for g in range(HIDDEN_PASSES):
+                acc = psum.tile([P, BANK], F32, tag="bank")
+                for f in range(FILTERS):
+                    nc.tensor.matmul_mx(
+                        out=acc[:],
+                        lhsT=perception_words[tile_no][:, f, :].bitcast(FP8X4),
+                        lhsT_scale=perception_scales[tile_no][:, f, :],
+                        rhs=wh_words[g][:, f, :].bitcast(FP8X4),
+                        rhs_scale=wh_planes[4 * f : P, g * BANK : (g + 1) * BANK],
+                        start=(f == 0),
+                        stop=(f == FILTERS - 1),
+                    )
+                nc.scalar.activation(
+                    out=rows[:, g].rearrange("q u (p e) -> q u p e", e=PAIR),
+                    in_=acc[:].rearrange("q (p u e) -> q u p e", u=PAIR, e=PAIR),
+                    func=RELU,
+                )
+            hidden_rows[tile_no] = rows
+
+        def transpose_hidden(tile_no):
+            hidden = work.tile([P, HIDDEN_PASSES, P, PACK], BF16, align_bytes=64)
+            passes_in_bank = BANK // (PAIR * P)
+            for first in range(0, HIDDEN_PASSES, passes_in_bank):
+                bank = psum.tile([P, passes_in_bank, PAIR, P], F32, tag="bank")
+                for g in range(passes_in_bank):
+                    for u in range(PAIR):
+                        nc.tensor.transpose(
+                            bank[:, g, u, :], hidden_rows[tile_no][:, first + g, u, :].bitcast(F32), ident_f32[:]
+                        )
+                nc.vector.tensor_copy(
+                    out=hidden[:, first : first + passes_in_bank].bitcast(F32),
+                    in_=bank[:].rearrange("p g u q -> p g q u"),
+                )
+            words = work.tile([P, HIDDEN_PASSES, P], U32, align_bytes=64)
+            scales = work.tile([P, HIDDEN_PASSES, P], U8, align_bytes=64)
+            nc.vector.quantize_mx(
+                out=words[:].rearrange("p g q -> p (g q)").bitcast(FP8X4),
+                scales=scales[:].rearrange("p g q -> p (g q)"),
+                in_=hidden[:].rearrange("p g q t -> p (g q t)"),
+            )
+            hidden_words[tile_no] = words
+            hidden_scales[tile_no] = scales
+
+        def second_layer(tile_no):
+            acc = psum.tile([P, CHANNELS], F32, tag="bank")
+            for g in range(HIDDEN_PASSES):
+                nc.tensor.matmul_mx(
+                    out=acc[:],
+                    lhsT=hidden_words[tile_no][:, g, :].bitcast(FP8X4),
+                    lhsT_scale=hidden_scales[tile_no][:, g, :],
+                    rhs=wo_words[:, g, :].bitcast(FP8X4),
+                    rhs_scale=wo_planes[4 * g : P, :],
+                    start=(g == 0),
+                    stop=(g == HIDDEN_PASSES - 1),
+                )
+            result = work.tile([P, CHANNELS], F32)
+            nc.scalar.copy(out=result[:], in_=acc[:])
+            nc.sync.dma_start(out=out_rows[tile_no * P : (tile_no + 1) * P, :], in_=result[:])
+
+        def sort_image_that_starts_at(tile_no):
+            if tile_no < PIXEL_TILES and tile_no % HALVES == 0:
+                sort_channels(tile_no // HALVES)
+
+        for tile_no in range(LEAD + 1):
+            sort_image_that_starts_at(tile_no)
+        for tile_no in range(LEAD):
+            filter_tile(tile_no)
+            quantise_perception(tile_no)
+        for r in range(PIXEL_TILES + 1):
+            sort_image_that_starts_at(r + LEAD + 1)
+            if r + LEAD < PIXEL_TILES:
+                filter_tile(r + LEAD)
+            if r > 0:
+                transpose_hidden(r - 1)
+            if r + LEAD < PIXEL_TILES:
+                quantise_perception(r + LEAD)
+            if r < PIXEL_TILES:
+                first_layer(r)
+            if r > 0:
+                second_layer(r - 1)

@@ -19,6 +19,7 @@ BANK = 512
 
 IMAGES, SIDE, CHANNELS, HIDDEN = 4, 16, 512, 2048
 HALVES = SIDE * SIDE // P
+TILE_ROWS = SIDE // HALVES
 PIXEL_TILES = IMAGES * HALVES
 FILTERS = 3
 HIDDEN_PASSES = HIDDEN // K_PASS
@@ -87,7 +88,7 @@ def tile_nn_kernel(tc, state_grid, w_hidden_words, w_hidden_scales, w_out_words,
         shifted = keep.tile([P, PADDED, PADDED], BF16)
         nc.vector.memset(shifted[:], 0.0)
         nc.vector.tensor_copy(
-            out=shifted[:, 1 : 1 + SIDE // HALVES, 1 : 1 + SIDE],
+            out=shifted[:, 1 : 1 + TILE_ROWS, 1 : 1 + SIDE],
             in_=ident_bf16[:].rearrange("k (i j) -> k i j", j=SIDE),
         )
         nc.vector.tensor_copy(out=shifted[:, SIDE + 1 :, 1 : 1 + SIDE], in_=shifted[:, 1:2, 1 : 1 + SIDE])
@@ -128,21 +129,30 @@ def tile_nn_kernel(tc, state_grid, w_hidden_words, w_hidden_scales, w_out_words,
             nc.scalar.copy(out=by_t[:], in_=state[b][:].rearrange("q half (p t) -> q half t p", t=PACK))
             sorted_state[b] = by_t
 
+        def edge_rows(pixels):
+            return pixels.rearrange("k (i j) -> k i j", j=SIDE)[:, 0 : TILE_ROWS : TILE_ROWS - 1, :]
+
         def filter_tile(tile_no):
             b, half = divmod(tile_no, HALVES)
             perception = work.tile([P, FILTERS, P, PACK], BF16, align_bytes=64)
             for f in range(FILTERS):
-                sources = (half,) if f == FILTERS - 1 else tuple(range(HALVES))
+                reaches_out = f < FILTERS - 1
                 bank = psum.tile([P, PACK, P], F32, tag="bank")
                 for t in range(PACK):
-                    for source in sources:
-                        own_or_other = (half - source) % HALVES
+                    nc.tensor.matmul(
+                        out=bank[:, t, :],
+                        lhsT=sorted_state[b][:, half, t, :],
+                        rhs=taps[:, f, :P],
+                        start=True,
+                        stop=not reaches_out,
+                    )
+                    if reaches_out:
                         nc.tensor.matmul(
-                            out=bank[:, t, :],
-                            lhsT=sorted_state[b][:, source, t, :],
-                            rhs=taps[:, f, own_or_other * P : (own_or_other + 1) * P],
-                            start=(source == sources[0]),
-                            stop=(source == sources[-1]),
+                            out=edge_rows(bank[:, t, :]),
+                            lhsT=sorted_state[b][:, 1 - half, t, :],
+                            rhs=edge_rows(taps[:, f, P:]),
+                            start=False,
+                            stop=True,
                         )
                 nc.vector.tensor_copy(out=perception[:, f], in_=bank[:].rearrange("p t q -> p q t"))
             grouped_perception[tile_no] = perception
@@ -182,25 +192,23 @@ def tile_nn_kernel(tc, state_grid, w_hidden_words, w_hidden_scales, w_out_words,
 
         def transpose_hidden(tile_no):
             hidden = work.tile([P, HIDDEN_PASSES, P, PACK], BF16, align_bytes=64)
+            words = work.tile([P, HIDDEN_PASSES, P], U32, align_bytes=64)
+            scales = work.tile([P, HIDDEN_PASSES, P], U8, align_bytes=64)
             passes_in_bank = BANK // (PAIR * P)
             for first in range(0, HIDDEN_PASSES, passes_in_bank):
+                these = slice(first, first + passes_in_bank)
                 bank = psum.tile([P, passes_in_bank, PAIR, P], F32, tag="bank")
                 for g in range(passes_in_bank):
                     for u in range(PAIR):
                         nc.tensor.transpose(
                             bank[:, g, u, :], hidden_rows[tile_no][:, first + g, u, :].bitcast(F32), ident_f32[:]
                         )
-                nc.vector.tensor_copy(
-                    out=hidden[:, first : first + passes_in_bank].bitcast(F32),
-                    in_=bank[:].rearrange("p g u q -> p g q u"),
+                nc.vector.tensor_copy(out=hidden[:, these].bitcast(F32), in_=bank[:].rearrange("p g u q -> p g q u"))
+                nc.vector.quantize_mx(
+                    out=words[:, these].rearrange("p g q -> p (g q)").bitcast(FP8X4),
+                    scales=scales[:, these].rearrange("p g q -> p (g q)"),
+                    in_=hidden[:, these].rearrange("p g q t -> p (g q t)"),
                 )
-            words = work.tile([P, HIDDEN_PASSES, P], U32, align_bytes=64)
-            scales = work.tile([P, HIDDEN_PASSES, P], U8, align_bytes=64)
-            nc.vector.quantize_mx(
-                out=words[:].rearrange("p g q -> p (g q)").bitcast(FP8X4),
-                scales=scales[:].rearrange("p g q -> p (g q)"),
-                in_=hidden[:].rearrange("p g q t -> p (g q t)"),
-            )
             hidden_words[tile_no] = words
             hidden_scales[tile_no] = scales
 

@@ -26,7 +26,7 @@ HIDDEN_PASSES = HIDDEN // K_PASS
 PAIR = 2
 PADDED = SIDE + 2
 
-LEAD = 2
+GROUP = 2
 
 FLOPS = 2 * IMAGES * SIDE * SIDE * (FILTERS * CHANNELS * HIDDEN + HIDDEN * CHANNELS)
 
@@ -39,7 +39,7 @@ def tile_nn_kernel(tc, state_grid, w_hidden_words, w_hidden_scales, w_out_words,
     with ExitStack() as stack:
         stack.enter_context(tc.manual_schedule())
         keep = stack.enter_context(tc.tile_pool(name="keep", bufs=1))
-        work = stack.enter_context(tc.tile_pool(name="work", bufs=2))
+        work = stack.enter_context(tc.tile_pool(name="work", bufs=2 * GROUP))
         psum = stack.enter_context(tc.psum_pool(name="psum", bufs=8))
 
         wh_planes = keep.tile([P, HIDDEN], U8, align_bytes=64)
@@ -61,7 +61,7 @@ def tile_nn_kernel(tc, state_grid, w_hidden_words, w_hidden_scales, w_out_words,
                     in_=scales[:, 4 * quadrant : 4 * quadrant + 4, :].bitcast(I32),
                 )
 
-        state = [load_image(b) for b in range(2)]
+        state = [load_image(b) for b in range(IMAGES)]
         load_planes(wh_planes, w_hidden_scales)
         wh_bytes = w_hidden_words.rearrange("f p n t -> p f (n t)")
         wh_words = []
@@ -72,7 +72,6 @@ def tile_nn_kernel(tc, state_grid, w_hidden_words, w_hidden_scales, w_out_words,
                 in_=wh_bytes[:, :, g * BANK * PACK : (g + 1) * BANK * PACK].bitcast(I32),
             )
             wh_words.append(block)
-        state.extend([load_image(b) for b in range(2, IMAGES)])
         load_planes(wo_planes, w_out_scales)
         wo_words = keep.tile([P, HIDDEN_PASSES, CHANNELS], U32, align_bytes=64)
         nc.sync.dma_start(
@@ -126,7 +125,14 @@ def tile_nn_kernel(tc, state_grid, w_hidden_words, w_hidden_scales, w_out_words,
 
         def sort_channels(b):
             by_t = keep.tile([P, HALVES, PACK, P], BF16, name="sorted%d" % b)
-            nc.scalar.copy(out=by_t[:], in_=state[b][:].rearrange("q half (p t) -> q half t p", t=PACK))
+            nc.gpsimd.tensor_scalar(
+                out=by_t[:],
+                in0=state[b][:].rearrange("q half (p t) -> q half t p", t=PACK),
+                scalar1=1.0,
+                scalar2=0.0,
+                op0=ALU.mult,
+                op1=ALU.add,
+            )
             sorted_state[b] = by_t
 
         def edge_rows(pixels):
@@ -154,7 +160,11 @@ def tile_nn_kernel(tc, state_grid, w_hidden_words, w_hidden_scales, w_out_words,
                             start=False,
                             stop=True,
                         )
-                nc.vector.tensor_copy(out=perception[:, f], in_=bank[:].rearrange("p t q -> p q t"))
+                side_by_side = bank[:].rearrange("p t q -> p q t")
+                if reaches_out:
+                    nc.scalar.copy(out=perception[:, f], in_=side_by_side)
+                else:
+                    nc.vector.tensor_copy(out=perception[:, f], in_=side_by_side)
             grouped_perception[tile_no] = perception
 
         def quantise_perception(tile_no):
@@ -228,24 +238,18 @@ def tile_nn_kernel(tc, state_grid, w_hidden_words, w_hidden_scales, w_out_words,
             nc.scalar.copy(out=result[:], in_=acc[:])
             nc.sync.dma_start(out=out_rows[tile_no * P : (tile_no + 1) * P, :], in_=result[:])
 
-        def sort_image_that_starts_at(tile_no):
-            if tile_no < PIXEL_TILES and tile_no % HALVES == 0:
-                sort_channels(tile_no // HALVES)
-
-        for tile_no in range(LEAD + 1):
-            sort_image_that_starts_at(tile_no)
-        for tile_no in range(LEAD):
+        sort_channels(0)
+        for tile_no in range(PIXEL_TILES):
+            if tile_no % HALVES == HALVES - 1 and tile_no + 1 < PIXEL_TILES:
+                sort_channels((tile_no + 1) // HALVES)
             filter_tile(tile_no)
             quantise_perception(tile_no)
-        for r in range(PIXEL_TILES + 1):
-            sort_image_that_starts_at(r + LEAD + 1)
-            if r + LEAD < PIXEL_TILES:
-                filter_tile(r + LEAD)
-            if r > 0:
-                transpose_hidden(r - 1)
-            if r + LEAD < PIXEL_TILES:
-                quantise_perception(r + LEAD)
-            if r < PIXEL_TILES:
-                first_layer(r)
-            if r > 0:
-                second_layer(r - 1)
+
+        groups = [range(first, first + GROUP) for first in range(0, PIXEL_TILES, GROUP)]
+        for now, before in zip(groups + [[]], [[]] + groups):
+            for tile_no in before:
+                transpose_hidden(tile_no)
+            for tile_no in now:
+                first_layer(tile_no)
+            for tile_no in before:
+                second_layer(tile_no)

@@ -18,17 +18,19 @@ K_PASS = P * PACK
 BANK = 512
 
 IMAGES, SIDE, CHANNELS, HIDDEN = 4, 16, 512, 2048
-HALVES = SIDE * SIDE // P
+IMAGE = SIDE * SIDE
+HALVES = IMAGE // P
 TILE_ROWS = SIDE // HALVES
-PIXEL_TILES = IMAGES * HALVES
 FILTERS = 3
 HIDDEN_PASSES = HIDDEN // K_PASS
 PAIR = 2
+LINE = 4
 PADDED = SIDE + 2
 
-GROUP = 2
+FILTER_BANKS = [(0, 0), (0, 2), (0, 1), (1, 2), (1, 0), (1, 1)]
+HEAD_FILL = 2
 
-FLOPS = 2 * IMAGES * SIDE * SIDE * (FILTERS * CHANNELS * HIDDEN + HIDDEN * CHANNELS)
+FLOPS = 2 * IMAGES * IMAGE * (FILTERS * CHANNELS * HIDDEN + HIDDEN * CHANNELS)
 
 
 def tile_nn_kernel(tc, state_grid, w_hidden_words, w_hidden_scales, w_out_words, w_out_scales, out):
@@ -39,17 +41,18 @@ def tile_nn_kernel(tc, state_grid, w_hidden_words, w_hidden_scales, w_out_words,
     with ExitStack() as stack:
         stack.enter_context(tc.manual_schedule())
         keep = stack.enter_context(tc.tile_pool(name="keep", bufs=1))
-        work = stack.enter_context(tc.tile_pool(name="work", bufs=2 * GROUP))
-        psum = stack.enter_context(tc.psum_pool(name="psum", bufs=8))
+        work = stack.enter_context(tc.tile_pool(name="work", bufs=2))
+        banks = stack.enter_context(tc.psum_pool(name="banks", bufs=6))
+        sums = stack.enter_context(tc.psum_pool(name="sums", bufs=2))
 
-        wh_planes = keep.tile([P, HIDDEN], U8, align_bytes=64)
+        wh_planes_raw = keep.tile([P, HIDDEN], U8, align_bytes=64)
         wo_planes = keep.tile([P, CHANNELS], U8, align_bytes=64)
-        nc.vector.memset(wh_planes[:].bitcast(I32), 0)
+        nc.vector.memset(wh_planes_raw[:].bitcast(I32), 0)
         nc.vector.memset(wo_planes[:].bitcast(I32), 0)
 
         def load_image(b):
             raw = keep.tile([P, HALVES, CHANNELS], BF16, name="state%d" % b)
-            rows = state_rows[b * HALVES * P : (b + 1) * HALVES * P, :]
+            rows = state_rows[b * IMAGE : (b + 1) * IMAGE, :]
             nc.sync.dma_start(out=raw[:], in_=rows.rearrange("(half q) c -> q half c", q=P))
             return raw
 
@@ -61,28 +64,30 @@ def tile_nn_kernel(tc, state_grid, w_hidden_words, w_hidden_scales, w_out_words,
                     in_=scales[:, 4 * quadrant : 4 * quadrant + 4, :].bitcast(I32),
                 )
 
-        state = [load_image(b) for b in range(IMAGES)]
-        load_planes(wh_planes, w_hidden_scales)
+        state = {}
+        state[0] = load_image(0)
+        state[1] = load_image(1)
+        load_planes(wh_planes_raw, w_hidden_scales)
         wh_bytes = w_hidden_words.rearrange("f p n t -> p f (n t)")
-        wh_words = []
+        wh_raw = []
         for g in range(HIDDEN_PASSES):
-            block = keep.tile([P, FILTERS, BANK], U32, name="wh_words%d" % g, align_bytes=64)
+            block = keep.tile([P, FILTERS, BANK], U32, name="wh_raw%d" % g, align_bytes=64)
             nc.sync.dma_start(
                 out=block[:].bitcast(I32),
                 in_=wh_bytes[:, :, g * BANK * PACK : (g + 1) * BANK * PACK].bitcast(I32),
             )
-            wh_words.append(block)
+            wh_raw.append(block)
         load_planes(wo_planes, w_out_scales)
         wo_words = keep.tile([P, HIDDEN_PASSES, CHANNELS], U32, align_bytes=64)
         nc.sync.dma_start(
             out=wo_words[:].bitcast(I32),
             in_=w_out_words.rearrange("g p n t -> p g (n t)").bitcast(I32),
         )
+        state[2] = load_image(2)
+        state[3] = load_image(3)
 
         ident_bf16 = keep.tile([P, P], BF16)
         make_identity(nc, ident_bf16[:])
-        ident_f32 = keep.tile([P, P], F32)
-        make_identity(nc, ident_f32[:])
 
         shifted = keep.tile([P, PADDED, PADDED], BF16)
         nc.vector.memset(shifted[:], 0.0)
@@ -115,13 +120,30 @@ def tile_nn_kernel(tc, state_grid, w_hidden_words, w_hidden_scales, w_out_words,
         )
         nc.vector.tensor_copy(out=taps[:, 2, :P], in_=ident_bf16[:])
 
+        wh_planes = keep.tile([P, HIDDEN], U8, align_bytes=64)
+        wh_words = {}
         sorted_state = {}
-        grouped_perception = {}
+        perception = {}
         perception_words = {}
         perception_scales = {}
-        hidden_rows = {}
+        hidden = {}
         hidden_words = {}
         hidden_scales = {}
+        out_sums = {}
+
+        def sort_hidden_units(g):
+            columns = slice(g * BANK, (g + 1) * BANK)
+            nc.vector.tensor_copy(
+                out=wh_planes[:, columns].rearrange("r (t m) -> r t m", t=PACK),
+                in_=wh_planes_raw[:, columns].rearrange("r (m t) -> r t m", t=PACK),
+            )
+            by_t = keep.tile([P, FILTERS, PACK, P], U32, name="wh_words%d" % g, align_bytes=64)
+            for f in range(FILTERS):
+                nc.vector.tensor_copy(
+                    out=by_t[:, f].bitcast(I32).rearrange("k t (c i) -> k c t i", i=LINE),
+                    in_=wh_raw[g][:, f, :].bitcast(I32).rearrange("k (c i t) -> k c t i", i=LINE, t=PACK),
+                )
+            wh_words[g] = by_t
 
         def sort_channels(b):
             by_t = keep.tile([P, HALVES, PACK, P], BF16, name="sorted%d" % b)
@@ -138,118 +160,149 @@ def tile_nn_kernel(tc, state_grid, w_hidden_words, w_hidden_scales, w_out_words,
         def edge_rows(pixels):
             return pixels.rearrange("k (i j) -> k i j", j=SIDE)[:, 0 : TILE_ROWS : TILE_ROWS - 1, :]
 
-        def filter_tile(tile_no):
-            b, half = divmod(tile_no, HALVES)
-            perception = work.tile([P, FILTERS, P, PACK], BF16, align_bytes=64)
-            for f in range(FILTERS):
-                reaches_out = f < FILTERS - 1
-                bank = psum.tile([P, PACK, P], F32, tag="bank")
-                for t in range(PACK):
-                    nc.tensor.matmul(
-                        out=bank[:, t, :],
-                        lhsT=sorted_state[b][:, half, t, :],
-                        rhs=taps[:, f, :P],
-                        start=True,
-                        stop=not reaches_out,
-                    )
-                    if reaches_out:
-                        nc.tensor.matmul(
-                            out=edge_rows(bank[:, t, :]),
-                            lhsT=sorted_state[b][:, 1 - half, t, :],
-                            rhs=edge_rows(taps[:, f, P:]),
-                            start=False,
-                            stop=True,
-                        )
-                side_by_side = bank[:].rearrange("p t q -> p q t")
-                if reaches_out:
-                    nc.scalar.copy(out=perception[:, f], in_=side_by_side)
-                else:
-                    nc.vector.tensor_copy(out=perception[:, f], in_=side_by_side)
-            grouped_perception[tile_no] = perception
-
-        def quantise_perception(tile_no):
-            words = keep.tile([P, FILTERS, P], U32, name="perception_words%d" % tile_no, align_bytes=64)
-            scales = keep.tile([P, FILTERS, P], U8, name="perception_scales%d" % tile_no, align_bytes=64)
-            for f in range(FILTERS):
-                nc.vector.quantize_mx(
-                    out=words[:, f, :].bitcast(FP8X4),
-                    scales=scales[:, f, :],
-                    in_=grouped_perception[tile_no][:, f].rearrange("p q t -> p (q t)"),
+        def filter_bank(b, half, f, on_scalar):
+            if b not in perception:
+                perception[b] = work.tile(
+                    [P, FILTERS, IMAGE, PACK], BF16, name="perception%d" % b, tag="perception", align_bytes=64
                 )
-            perception_words[tile_no] = words
-            perception_scales[tile_no] = scales
+            reaches_out = f < FILTERS - 1
+            bank = banks.tile([P, PACK, P], F32, tag="bank")
+            for t in range(PACK):
+                nc.tensor.matmul(
+                    out=bank[:, t, :],
+                    lhsT=sorted_state[b][:, half, t, :],
+                    rhs=taps[:, f, :P],
+                    start=True,
+                    stop=not reaches_out,
+                )
+                if reaches_out:
+                    nc.tensor.matmul(
+                        out=edge_rows(bank[:, t, :]),
+                        lhsT=sorted_state[b][:, 1 - half, t, :],
+                        rhs=edge_rows(taps[:, f, P:]),
+                        start=False,
+                        stop=True,
+                    )
+            side_by_side = bank[:].rearrange("p t q -> p q t")
+            place = perception[b][:, f, half * P : (half + 1) * P, :]
+            if on_scalar:
+                nc.scalar.copy(out=place, in_=side_by_side)
+            else:
+                nc.vector.tensor_copy(out=place, in_=side_by_side)
 
-        def first_layer(tile_no):
-            rows = work.tile([P, HIDDEN_PASSES, PAIR, P * PAIR], BF16)
-            for g in range(HIDDEN_PASSES):
-                acc = psum.tile([P, BANK], F32, tag="bank")
+        def quantise_perception(b, f):
+            if b not in perception_words:
+                perception_words[b] = keep.tile(
+                    [P, FILTERS, IMAGE], U32, name="perception_words%d" % b, align_bytes=64
+                )
+                perception_scales[b] = keep.tile(
+                    [P, FILTERS, IMAGE], U8, name="perception_scales%d" % b, align_bytes=64
+                )
+            nc.vector.quantize_mx(
+                out=perception_words[b][:, f, :].bitcast(FP8X4),
+                scales=perception_scales[b][:, f, :],
+                in_=perception[b][:, f].rearrange("p q t -> p (q t)"),
+            )
+
+        def first_layer(b, g, u):
+            if b not in hidden:
+                hidden[b] = work.tile(
+                    [P, HIDDEN_PASSES, IMAGE, PACK], BF16, name="hidden%d" % b, tag="hidden", align_bytes=64
+                )
+            bank = banks.tile([P, PAIR, IMAGE], F32, tag="bank")
+            for e in range(PAIR):
+                t = PAIR * u + e
+                first = (g * PACK + t) * P
                 for f in range(FILTERS):
                     nc.tensor.matmul_mx(
-                        out=acc[:],
-                        lhsT=perception_words[tile_no][:, f, :].bitcast(FP8X4),
-                        lhsT_scale=perception_scales[tile_no][:, f, :],
-                        rhs=wh_words[g][:, f, :].bitcast(FP8X4),
-                        rhs_scale=wh_planes[4 * f : P, g * BANK : (g + 1) * BANK],
+                        out=bank[:, e, :],
+                        lhsT=wh_words[g][:, f, t, :].bitcast(FP8X4),
+                        lhsT_scale=wh_planes[4 * f : P, first : first + P],
+                        rhs=perception_words[b][:, f, :].bitcast(FP8X4),
+                        rhs_scale=perception_scales[b][:, f, :],
                         start=(f == 0),
                         stop=(f == FILTERS - 1),
                     )
-                nc.scalar.activation(
-                    out=rows[:, g].rearrange("q u (p e) -> q u p e", e=PAIR),
-                    in_=acc[:].rearrange("q (p u e) -> q u p e", u=PAIR, e=PAIR),
-                    func=RELU,
-                )
-            hidden_rows[tile_no] = rows
+            place = hidden[b][:, g, :, PAIR * u : PAIR * (u + 1)]
+            side_by_side = bank[:].rearrange("p e q -> p q e")
+            if u == 0:
+                nc.vector.tensor_scalar_max(out=place, in0=side_by_side, scalar1=0.0)
+            else:
+                nc.scalar.activation(out=place, in_=side_by_side, func=RELU)
 
-        def transpose_hidden(tile_no):
-            hidden = work.tile([P, HIDDEN_PASSES, P, PACK], BF16, align_bytes=64)
-            words = work.tile([P, HIDDEN_PASSES, P], U32, align_bytes=64)
-            scales = work.tile([P, HIDDEN_PASSES, P], U8, align_bytes=64)
-            passes_in_bank = BANK // (PAIR * P)
-            for first in range(0, HIDDEN_PASSES, passes_in_bank):
-                these = slice(first, first + passes_in_bank)
-                bank = psum.tile([P, passes_in_bank, PAIR, P], F32, tag="bank")
-                for g in range(passes_in_bank):
-                    for u in range(PAIR):
-                        nc.tensor.transpose(
-                            bank[:, g, u, :], hidden_rows[tile_no][:, first + g, u, :].bitcast(F32), ident_f32[:]
-                        )
-                nc.vector.tensor_copy(out=hidden[:, these].bitcast(F32), in_=bank[:].rearrange("p g u q -> p g q u"))
-                nc.vector.quantize_mx(
-                    out=words[:, these].rearrange("p g q -> p (g q)").bitcast(FP8X4),
-                    scales=scales[:, these].rearrange("p g q -> p (g q)"),
-                    in_=hidden[:, these].rearrange("p g q t -> p (g q t)"),
+        def quantise_hidden(b, g):
+            if b not in hidden_words:
+                hidden_words[b] = work.tile(
+                    [P, HIDDEN_PASSES, IMAGE], U32, name="hidden_words%d" % b, tag="hidden_words", align_bytes=64
                 )
-            hidden_words[tile_no] = words
-            hidden_scales[tile_no] = scales
+                hidden_scales[b] = work.tile(
+                    [P, HIDDEN_PASSES, IMAGE], U8, name="hidden_scales%d" % b, tag="hidden_scales", align_bytes=64
+                )
+            nc.vector.quantize_mx(
+                out=hidden_words[b][:, g, :].bitcast(FP8X4),
+                scales=hidden_scales[b][:, g, :],
+                in_=hidden[b][:, g].rearrange("p q t -> p (q t)"),
+            )
 
-        def second_layer(tile_no):
-            acc = psum.tile([P, CHANNELS], F32, tag="bank")
-            for g in range(HIDDEN_PASSES):
+        def second_layer(b, g):
+            for half in range(HALVES):
+                if g == 0:
+                    out_sums[b, half] = sums.tile([P, CHANNELS], F32, name="sums%d_%d" % (b, half), tag="sums")
                 nc.tensor.matmul_mx(
-                    out=acc[:],
-                    lhsT=hidden_words[tile_no][:, g, :].bitcast(FP8X4),
-                    lhsT_scale=hidden_scales[tile_no][:, g, :],
+                    out=out_sums[b, half][:],
+                    lhsT=hidden_words[b][:, g, half * P : (half + 1) * P].bitcast(FP8X4),
+                    lhsT_scale=hidden_scales[b][:, g, half * P : (half + 1) * P],
                     rhs=wo_words[:, g, :].bitcast(FP8X4),
                     rhs_scale=wo_planes[4 * g : P, :],
                     start=(g == 0),
                     stop=(g == HIDDEN_PASSES - 1),
                 )
-            result = work.tile([P, CHANNELS], F32)
-            nc.scalar.copy(out=result[:], in_=acc[:])
-            nc.sync.dma_start(out=out_rows[tile_no * P : (tile_no + 1) * P, :], in_=result[:])
+
+        def store(b, half, on_scalar):
+            result = work.tile([P, CHANNELS], F32, name="result%d_%d" % (b, half), tag="result", bufs=4)
+            if on_scalar:
+                nc.scalar.copy(out=result[:], in_=out_sums[b, half][:])
+            else:
+                nc.vector.tensor_copy(out=result[:], in_=out_sums[b, half][:])
+            first = (b * HALVES + half) * P
+            nc.sync.dma_start(out=out_rows[first : first + P, :], in_=result[:])
 
         sort_channels(0)
-        for tile_no in range(PIXEL_TILES):
-            if tile_no % HALVES == HALVES - 1 and tile_no + 1 < PIXEL_TILES:
-                sort_channels((tile_no + 1) // HALVES)
-            filter_tile(tile_no)
-            quantise_perception(tile_no)
+        sort_channels(1)
+        for n, (half, f) in enumerate(FILTER_BANKS):
+            filter_bank(0, half, f, on_scalar=(n % 2 == 1))
+            if n == 2:
+                sort_hidden_units(0)
+        for n in range(HEAD_FILL):
+            filter_bank(1, FILTER_BANKS[n][0], FILTER_BANKS[n][1], on_scalar=True)
+        for f in (2, 0, 1):
+            quantise_perception(0, f)
+        sort_hidden_units(1)
 
-        groups = [range(first, first + GROUP) for first in range(0, PIXEL_TILES, GROUP)]
-        for now, before in zip(groups + [[]], [[]] + groups):
-            for tile_no in before:
-                transpose_hidden(tile_no)
-            for tile_no in now:
-                first_layer(tile_no)
-            for tile_no in before:
-                second_layer(tile_no)
+        for b in range(IMAGES):
+            for g in range(HIDDEN_PASSES):
+                for u in range(PAIR):
+                    step = PAIR * g + u
+                    first_layer(b, g, u)
+                    n = step + (HEAD_FILL if b == 0 else 0)
+                    if b + 1 < IMAGES and n < len(FILTER_BANKS):
+                        filter_bank(b + 1, FILTER_BANKS[n][0], FILTER_BANKS[n][1], on_scalar=(u == 0 or b == 0))
+                if g == 0 and b > 0:
+                    second_layer(b - 1, HIDDEN_PASSES - 1)
+                    store(b - 1, 0, on_scalar=True)
+                    store(b - 1, 1, on_scalar=True)
+                if g > 0:
+                    second_layer(b, g - 1)
+                if b == 0 and g + 2 < HIDDEN_PASSES:
+                    sort_hidden_units(g + 2)
+                if b + 2 < IMAGES and g == 1:
+                    sort_channels(b + 2)
+                if b + 1 < IMAGES and g == 2:
+                    quantise_perception(b + 1, 2)
+                    quantise_perception(b + 1, 0)
+                if b + 1 < IMAGES and g == 3:
+                    quantise_perception(b + 1, 1)
+                quantise_hidden(b, g)
+        second_layer(IMAGES - 1, HIDDEN_PASSES - 1)
+        store(IMAGES - 1, 0, on_scalar=True)
+        store(IMAGES - 1, 1, on_scalar=False)

@@ -27,8 +27,10 @@ PAIR = 2
 LINE = 4
 PADDED = SIDE + 2
 
-FILTER_BANKS = [(0, 0), (0, 2), (0, 1), (1, 2), (1, 0), (1, 1)]
+FILTER_BANKS = [(0, 2), (1, 2), (0, 0), (1, 0), (0, 1), (1, 1)]
+PASS_ORDER = (2, 0, 1)
 HEAD_FILL = 2
+LAG = 2
 
 FLOPS = 2 * IMAGES * IMAGE * (FILTERS * CHANNELS * HIDDEN + HIDDEN * CHANNELS)
 
@@ -99,7 +101,7 @@ def tile_nn_kernel(tc, state_grid, w_hidden_words, w_hidden_scales, w_out_words,
         nc.vector.tensor_copy(out=shifted[:, :, 0:1], in_=shifted[:, :, SIDE : SIDE + 1])
         nc.vector.tensor_copy(out=shifted[:, :, SIDE + 1 :], in_=shifted[:, :, 1:2])
 
-        taps = keep.tile([P, FILTERS, HALVES * P], BF16)
+        taps = keep.tile([P, FILTERS - 1, HALVES * P], BF16)
         diff_x = keep.tile([P, PADDED, SIDE], BF16)
         nc.vector.tensor_sub(out=diff_x[:], in0=shifted[:, :, 2:], in1=shifted[:, :, :SIDE])
         part_x = keep.tile([P, SIDE, SIDE], BF16)
@@ -118,7 +120,6 @@ def tile_nn_kernel(tc, state_grid, w_hidden_words, w_hidden_scales, w_out_words,
         nc.vector.tensor_add(
             out=taps[:, 1, :].rearrange("k (i j) -> k i j", j=SIDE), in0=part_y[:], in1=diff_y[:, :, 2:]
         )
-        nc.vector.tensor_copy(out=taps[:, 2, :P], in_=ident_bf16[:])
 
         wh_planes = keep.tile([P, HIDDEN], U8, align_bytes=64)
         wh_words = {}
@@ -145,16 +146,15 @@ def tile_nn_kernel(tc, state_grid, w_hidden_words, w_hidden_scales, w_out_words,
                 )
             wh_words[g] = by_t
 
-        def sort_channels(b):
+        def sort_channels(b, on_scalar):
             by_t = keep.tile([P, HALVES, PACK, P], BF16, name="sorted%d" % b)
-            nc.gpsimd.tensor_scalar(
-                out=by_t[:],
-                in0=state[b][:].rearrange("q half (p t) -> q half t p", t=PACK),
-                scalar1=1.0,
-                scalar2=0.0,
-                op0=ALU.mult,
-                op1=ALU.add,
-            )
+            for half in range(HALVES):
+                together = by_t[:, half].rearrange("q t (c i) -> q c t i", i=2 * LINE)
+                as_loaded = state[b][:, half, :].rearrange("q (c i t) -> q c t i", i=2 * LINE, t=PACK)
+                if on_scalar:
+                    nc.scalar.copy(out=together, in_=as_loaded)
+                else:
+                    nc.vector.tensor_copy(out=together, in_=as_loaded)
             sorted_state[b] = by_t
 
         def edge_rows(pixels):
@@ -171,7 +171,7 @@ def tile_nn_kernel(tc, state_grid, w_hidden_words, w_hidden_scales, w_out_words,
                 nc.tensor.matmul(
                     out=bank[:, t, :],
                     lhsT=sorted_state[b][:, half, t, :],
-                    rhs=taps[:, f, :P],
+                    rhs=(taps[:, f, :P] if reaches_out else ident_bf16[:]),
                     start=True,
                     stop=not reaches_out,
                 )
@@ -213,15 +213,15 @@ def tile_nn_kernel(tc, state_grid, w_hidden_words, w_hidden_scales, w_out_words,
             for e in range(PAIR):
                 t = PAIR * u + e
                 first = (g * PACK + t) * P
-                for f in range(FILTERS):
+                for f in PASS_ORDER:
                     nc.tensor.matmul_mx(
                         out=bank[:, e, :],
                         lhsT=wh_words[g][:, f, t, :].bitcast(FP8X4),
                         lhsT_scale=wh_planes[4 * f : P, first : first + P],
                         rhs=perception_words[b][:, f, :].bitcast(FP8X4),
                         rhs_scale=perception_scales[b][:, f, :],
-                        start=(f == 0),
-                        stop=(f == FILTERS - 1),
+                        start=(f == PASS_ORDER[0]),
+                        stop=(f == PASS_ORDER[-1]),
                     )
             place = hidden[b][:, g, :, PAIR * u : PAIR * (u + 1)]
             side_by_side = bank[:].rearrange("p e q -> p q e")
@@ -267,15 +267,14 @@ def tile_nn_kernel(tc, state_grid, w_hidden_words, w_hidden_scales, w_out_words,
             first = (b * HALVES + half) * P
             nc.sync.dma_start(out=out_rows[first : first + P, :], in_=result[:])
 
-        sort_channels(0)
-        sort_channels(1)
+        sort_channels(0, on_scalar=True)
+        sort_channels(1, on_scalar=True)
         for n, (half, f) in enumerate(FILTER_BANKS):
-            filter_bank(0, half, f, on_scalar=(n % 2 == 1))
-            if n == 2:
-                sort_hidden_units(0)
+            filter_bank(0, half, f, on_scalar=(n not in (0, 2)))
         for n in range(HEAD_FILL):
             filter_bank(1, FILTER_BANKS[n][0], FILTER_BANKS[n][1], on_scalar=True)
-        for f in (2, 0, 1):
+        sort_hidden_units(0)
+        for f in PASS_ORDER:
             quantise_perception(0, f)
         sort_hidden_units(1)
 
@@ -287,22 +286,20 @@ def tile_nn_kernel(tc, state_grid, w_hidden_words, w_hidden_scales, w_out_words,
                     n = step + (HEAD_FILL if b == 0 else 0)
                     if b + 1 < IMAGES and n < len(FILTER_BANKS):
                         filter_bank(b + 1, FILTER_BANKS[n][0], FILTER_BANKS[n][1], on_scalar=(u == 0 or b == 0))
-                if g == 0 and b > 0:
-                    second_layer(b - 1, HIDDEN_PASSES - 1)
-                    store(b - 1, 0, on_scalar=True)
-                    store(b - 1, 1, on_scalar=True)
-                if g > 0:
-                    second_layer(b, g - 1)
+                behind = b * HIDDEN_PASSES + g - LAG
+                if behind >= 0:
+                    second_layer(behind // HIDDEN_PASSES, behind % HIDDEN_PASSES)
+                    if behind % HIDDEN_PASSES == HIDDEN_PASSES - 1:
+                        store(behind // HIDDEN_PASSES, 0, on_scalar=True)
+                        store(behind // HIDDEN_PASSES, 1, on_scalar=True)
                 if b == 0 and g + 2 < HIDDEN_PASSES:
                     sort_hidden_units(g + 2)
-                if b + 2 < IMAGES and g == 1:
-                    sort_channels(b + 2)
-                if b + 1 < IMAGES and g == 2:
-                    quantise_perception(b + 1, 2)
-                    quantise_perception(b + 1, 0)
-                if b + 1 < IMAGES and g == 3:
-                    quantise_perception(b + 1, 1)
+                if b + 2 < IMAGES and g == 2:
+                    sort_channels(b + 2, on_scalar=True)
+                if b + 1 < IMAGES and g > 0:
+                    quantise_perception(b + 1, PASS_ORDER[g - 1])
                 quantise_hidden(b, g)
-        second_layer(IMAGES - 1, HIDDEN_PASSES - 1)
+        for g in range(HIDDEN_PASSES - LAG, HIDDEN_PASSES):
+            second_layer(IMAGES - 1, g)
         store(IMAGES - 1, 0, on_scalar=True)
         store(IMAGES - 1, 1, on_scalar=False)

@@ -20,17 +20,27 @@ BANK = 512
 IMAGES, SIDE, CHANNELS, HIDDEN = 4, 16, 512, 2048
 IMAGE = SIDE * SIDE
 HALVES = IMAGE // P
-TILE_ROWS = SIDE // HALVES
+WINDOW_ROWS = P // SIDE
+INNER_ROWS = WINDOW_ROWS - 2
+WINDOWS = 3
+TOGETHER = 2
 FILTERS = 3
 HIDDEN_PASSES = HIDDEN // K_PASS
 PAIR = 2
 LINE = 4
 PADDED = SIDE + 2
 
-FILTER_BANKS = [(0, 2), (1, 2), (0, 0), (1, 0), (0, 1), (1, 1)]
+FILTER_STEPS = [
+    [(0, (2,)), (1, (2,))],
+    [(2, (2,))],
+    [(0, (0,)), (1, (0,))],
+    [(2, (0, 1))],
+    [(0, (1,))],
+    [(1, (1,))],
+]
 PASS_ORDER = (2, 0, 1)
-HEAD_FILL = 2
-LAG = 2
+HEAD_FILL = 6
+LAG = 3
 
 FLOPS = 2 * IMAGES * IMAGE * (FILTERS * CHANNELS * HIDDEN + HIDDEN * CHANNELS)
 
@@ -52,11 +62,21 @@ def tile_nn_kernel(tc, state_grid, w_hidden_words, w_hidden_scales, w_out_words,
         nc.vector.memset(wh_planes_raw[:].bitcast(I32), 0)
         nc.vector.memset(wo_planes[:].bitcast(I32), 0)
 
-        def load_image(b):
-            raw = keep.tile([P, HALVES, CHANNELS], BF16, name="state%d" % b)
-            rows = state_rows[b * IMAGE : (b + 1) * IMAGE, :]
-            nc.sync.dma_start(out=raw[:], in_=rows.rearrange("(half q) c -> q half c", q=P))
-            return raw
+        state = {}
+
+        def load_images(first_image):
+            raw = keep.tile([P, TOGETHER, WINDOWS, CHANNELS], BF16, name="state%d" % first_image)
+            rows = state_rows[first_image * IMAGE : (first_image + TOGETHER) * IMAGE, :].rearrange(
+                "(b q) c -> q b c", b=TOGETHER
+            )
+            for w in range(WINDOWS):
+                first = INNER_ROWS * w * SIDE
+                inside = min(P, IMAGE - first)
+                nc.sync.dma_start(out=raw[:inside, :, w, :], in_=rows[first : first + inside])
+                if inside < P:
+                    nc.sync.dma_start(out=raw[inside:, :, w, :], in_=rows[: P - inside])
+            for b in range(TOGETHER):
+                state[first_image + b] = raw[:, b]
 
         def load_planes(planes, scales):
             passes = scales.shape[0]
@@ -66,9 +86,7 @@ def tile_nn_kernel(tc, state_grid, w_hidden_words, w_hidden_scales, w_out_words,
                     in_=scales[:, 4 * quadrant : 4 * quadrant + 4, :].bitcast(I32),
                 )
 
-        state = {}
-        state[0] = load_image(0)
-        state[1] = load_image(1)
+        load_images(0)
         load_planes(wh_planes_raw, w_hidden_scales)
         wh_bytes = w_hidden_words.rearrange("f p n t -> p f (n t)")
         wh_raw = []
@@ -85,40 +103,39 @@ def tile_nn_kernel(tc, state_grid, w_hidden_words, w_hidden_scales, w_out_words,
             out=wo_words[:].bitcast(I32),
             in_=w_out_words.rearrange("g p n t -> p g (n t)").bitcast(I32),
         )
-        state[2] = load_image(2)
-        state[3] = load_image(3)
+        load_images(TOGETHER)
 
         ident_bf16 = keep.tile([P, P], BF16)
         make_identity(nc, ident_bf16[:])
 
-        shifted = keep.tile([P, PADDED, PADDED], BF16)
-        nc.vector.memset(shifted[:], 0.0)
-        nc.vector.tensor_copy(
-            out=shifted[:, 1 : 1 + TILE_ROWS, 1 : 1 + SIDE],
-            in_=ident_bf16[:].rearrange("k (i j) -> k i j", j=SIDE),
-        )
-        nc.vector.tensor_copy(out=shifted[:, SIDE + 1 :, 1 : 1 + SIDE], in_=shifted[:, 1:2, 1 : 1 + SIDE])
-        nc.vector.tensor_copy(out=shifted[:, :, 0:1], in_=shifted[:, :, SIDE : SIDE + 1])
-        nc.vector.tensor_copy(out=shifted[:, :, SIDE + 1 :], in_=shifted[:, :, 1:2])
+        padded = keep.tile([P, WINDOW_ROWS, PADDED], BF16)
+        nc.vector.tensor_copy(out=padded[:, :, 1 : 1 + SIDE], in_=ident_bf16[:].rearrange("k (a c) -> k a c", c=SIDE))
+        nc.vector.tensor_copy(out=padded[:, :, 0:1], in_=padded[:, :, SIDE : SIDE + 1])
+        nc.vector.tensor_copy(out=padded[:, :, SIDE + 1 :], in_=padded[:, :, 1:2])
 
-        taps = keep.tile([P, FILTERS - 1, HALVES * P], BF16)
-        diff_x = keep.tile([P, PADDED, SIDE], BF16)
-        nc.vector.tensor_sub(out=diff_x[:], in0=shifted[:, :, 2:], in1=shifted[:, :, :SIDE])
-        part_x = keep.tile([P, SIDE, SIDE], BF16)
+        taps = keep.tile([P, FILTERS - 1, INNER_ROWS * SIDE], BF16)
+        diff_x = keep.tile([P, WINDOW_ROWS, SIDE], BF16)
+        part_x = keep.tile([P, INNER_ROWS, SIDE], BF16)
+        part_y = keep.tile([P, WINDOW_ROWS, SIDE], BF16)
+        sum_y = keep.tile([P, WINDOW_ROWS, SIDE], BF16)
+        nc.vector.tensor_sub(out=diff_x[:], in0=padded[:, :, 2:], in1=padded[:, :, :SIDE])
         nc.vector.scalar_tensor_tensor(
-            out=part_x[:], in0=diff_x[:, 1 : 1 + SIDE, :], scalar=2.0, in1=diff_x[:, :SIDE, :], op0=ALU.mult, op1=ALU.add
+            out=part_y[:], in0=padded[:, :, 1 : 1 + SIDE], scalar=2.0, in1=padded[:, :, :SIDE], op0=ALU.mult, op1=ALU.add
         )
-        nc.vector.tensor_add(
-            out=taps[:, 0, :].rearrange("k (i j) -> k i j", j=SIDE), in0=part_x[:], in1=diff_x[:, 2:, :]
-        )
-        diff_y = keep.tile([P, SIDE, PADDED], BF16)
-        nc.vector.tensor_sub(out=diff_y[:], in0=shifted[:, 2:, :], in1=shifted[:, :SIDE, :])
-        part_y = keep.tile([P, SIDE, SIDE], BF16)
         nc.vector.scalar_tensor_tensor(
-            out=part_y[:], in0=diff_y[:, :, 1 : 1 + SIDE], scalar=2.0, in1=diff_y[:, :, :SIDE], op0=ALU.mult, op1=ALU.add
+            out=part_x[:],
+            in0=diff_x[:, 1 : 1 + INNER_ROWS, :],
+            scalar=2.0,
+            in1=diff_x[:, :INNER_ROWS, :],
+            op0=ALU.mult,
+            op1=ALU.add,
         )
+        nc.vector.tensor_add(out=sum_y[:], in0=part_y[:], in1=padded[:, :, 2:])
         nc.vector.tensor_add(
-            out=taps[:, 1, :].rearrange("k (i j) -> k i j", j=SIDE), in0=part_y[:], in1=diff_y[:, :, 2:]
+            out=taps[:, 0, :].rearrange("k (o j) -> k o j", j=SIDE), in0=part_x[:], in1=diff_x[:, 2:, :]
+        )
+        nc.vector.tensor_sub(
+            out=taps[:, 1, :].rearrange("k (o j) -> k o j", j=SIDE), in0=sum_y[:, 2:, :], in1=sum_y[:, :INNER_ROWS, :]
         )
 
         wh_planes = keep.tile([P, HIDDEN], U8, align_bytes=64)
@@ -139,52 +156,45 @@ def tile_nn_kernel(tc, state_grid, w_hidden_words, w_hidden_scales, w_out_words,
                 in_=wh_planes_raw[:, columns].rearrange("r (m t) -> r t m", t=PACK),
             )
             by_t = keep.tile([P, FILTERS, PACK, P], U32, name="wh_words%d" % g, align_bytes=64)
-            for f in range(FILTERS):
+            for f in PASS_ORDER:
                 nc.vector.tensor_copy(
                     out=by_t[:, f].bitcast(I32).rearrange("k t (c i) -> k c t i", i=LINE),
                     in_=wh_raw[g][:, f, :].bitcast(I32).rearrange("k (c i t) -> k c t i", i=LINE, t=PACK),
                 )
             wh_words[g] = by_t
 
-        def sort_channels(b, on_scalar):
-            by_t = keep.tile([P, HALVES, PACK, P], BF16, name="sorted%d" % b)
-            for half in range(HALVES):
-                together = by_t[:, half].rearrange("q t (c i) -> q c t i", i=2 * LINE)
-                as_loaded = state[b][:, half, :].rearrange("q (c i t) -> q c t i", i=2 * LINE, t=PACK)
-                if on_scalar:
-                    nc.scalar.copy(out=together, in_=as_loaded)
-                else:
-                    nc.vector.tensor_copy(out=together, in_=as_loaded)
-            sorted_state[b] = by_t
+        def sort_channels(b, w, engine):
+            if b not in sorted_state:
+                sorted_state[b] = keep.tile([P, WINDOWS, PACK, P], BF16, name="sorted%d" % b)
+            together = sorted_state[b][:, w].rearrange("q t (c i) -> q c t i", i=2 * LINE)
+            as_loaded = state[b][:, w, :].rearrange("q (c i t) -> q c t i", i=2 * LINE, t=PACK)
+            if engine == "scalar":
+                nc.scalar.copy(out=together, in_=as_loaded)
+            elif engine == "vector":
+                nc.vector.tensor_copy(out=together, in_=as_loaded)
+            else:
+                nc.gpsimd.tensor_scalar(
+                    out=together, in0=as_loaded, scalar1=1.0, scalar2=0.0, op0=ALU.mult, op1=ALU.add
+                )
 
-        def edge_rows(pixels):
-            return pixels.rearrange("k (i j) -> k i j", j=SIDE)[:, 0 : TILE_ROWS : TILE_ROWS - 1, :]
-
-        def filter_bank(b, half, f, on_scalar):
+        def filter_bank(b, w, filters, on_scalar):
             if b not in perception:
                 perception[b] = work.tile(
                     [P, FILTERS, IMAGE, PACK], BF16, name="perception%d" % b, tag="perception", align_bytes=64
                 )
-            reaches_out = f < FILTERS - 1
-            bank = banks.tile([P, PACK, P], F32, tag="bank")
+            first = INNER_ROWS * w * SIDE
+            width = min(INNER_ROWS * SIDE, IMAGE - first)
+            bank = banks.tile([P, PACK, len(filters), width], F32, tag="bank")
             for t in range(PACK):
                 nc.tensor.matmul(
-                    out=bank[:, t, :],
-                    lhsT=sorted_state[b][:, half, t, :],
-                    rhs=(taps[:, f, :P] if reaches_out else ident_bf16[:]),
+                    out=bank[:, t],
+                    lhsT=sorted_state[b][:, w, t, :],
+                    rhs=(ident_bf16[:, SIDE : SIDE + width] if filters[0] == FILTERS - 1 else taps[:, filters[0] : filters[-1] + 1, :width]),
                     start=True,
-                    stop=not reaches_out,
+                    stop=True,
                 )
-                if reaches_out:
-                    nc.tensor.matmul(
-                        out=edge_rows(bank[:, t, :]),
-                        lhsT=sorted_state[b][:, 1 - half, t, :],
-                        rhs=edge_rows(taps[:, f, P:]),
-                        start=False,
-                        stop=True,
-                    )
-            side_by_side = bank[:].rearrange("p t q -> p q t")
-            place = perception[b][:, f, half * P : (half + 1) * P, :]
+            side_by_side = bank[:].rearrange("p t f q -> p f q t")
+            place = perception[b][:, filters[0] : filters[-1] + 1, first : first + width, :]
             if on_scalar:
                 nc.scalar.copy(out=place, in_=side_by_side)
             else:
@@ -225,7 +235,7 @@ def tile_nn_kernel(tc, state_grid, w_hidden_words, w_hidden_scales, w_out_words,
                     )
             place = hidden[b][:, g, :, PAIR * u : PAIR * (u + 1)]
             side_by_side = bank[:].rearrange("p e q -> p q e")
-            if u == 0:
+            if u == 0 and b > 0:
                 nc.vector.tensor_scalar_max(out=place, in0=side_by_side, scalar1=0.0)
             else:
                 nc.scalar.activation(out=place, in_=side_by_side, func=RELU)
@@ -264,18 +274,32 @@ def tile_nn_kernel(tc, state_grid, w_hidden_words, w_hidden_scales, w_out_words,
                 nc.scalar.copy(out=result[:], in_=out_sums[b, half][:])
             else:
                 nc.vector.tensor_copy(out=result[:], in_=out_sums[b, half][:])
-            first = (b * HALVES + half) * P
-            nc.sync.dma_start(out=out_rows[first : first + P, :], in_=result[:])
+            first = b * IMAGE + half * P + SIDE
+            inside = min(P, (b + 1) * IMAGE - first)
+            nc.sync.dma_start(out=out_rows[first : first + inside, :], in_=result[:inside, :])
+            if inside < P:
+                nc.sync.dma_start(out=out_rows[b * IMAGE : b * IMAGE + P - inside, :], in_=result[inside:, :])
 
-        sort_channels(0, on_scalar=True)
-        sort_channels(1, on_scalar=True)
-        for n, (half, f) in enumerate(FILTER_BANKS):
-            filter_bank(0, half, f, on_scalar=(n not in (0, 2)))
+        sort_channels(0, 0, "scalar")
+        sort_channels(0, 1, "scalar")
+        sort_channels(0, 2, "vector")
+        for w in range(WINDOWS):
+            sort_channels(1, w, "gpsimd")
+        filter_bank(0, 0, (2,), on_scalar=True)
+        filter_bank(0, 1, (2,), on_scalar=False)
+        filter_bank(0, 2, (2,), on_scalar=True)
+        filter_bank(0, 0, (0,), on_scalar=False)
+        quantise_perception(0, 2)
+        filter_bank(0, 1, (0,), on_scalar=True)
+        filter_bank(0, 2, (0, 1), on_scalar=False)
+        filter_bank(0, 0, (1,), on_scalar=False)
+        filter_bank(0, 1, (1,), on_scalar=True)
+        quantise_perception(0, 0)
+        quantise_perception(0, 1)
         for n in range(HEAD_FILL):
-            filter_bank(1, FILTER_BANKS[n][0], FILTER_BANKS[n][1], on_scalar=True)
+            for window, filters in FILTER_STEPS[n]:
+                filter_bank(1, window, filters, on_scalar=True)
         sort_hidden_units(0)
-        for f in PASS_ORDER:
-            quantise_perception(0, f)
         sort_hidden_units(1)
 
         for b in range(IMAGES):
@@ -284,8 +308,9 @@ def tile_nn_kernel(tc, state_grid, w_hidden_words, w_hidden_scales, w_out_words,
                     step = PAIR * g + u
                     first_layer(b, g, u)
                     n = step + (HEAD_FILL if b == 0 else 0)
-                    if b + 1 < IMAGES and n < len(FILTER_BANKS):
-                        filter_bank(b + 1, FILTER_BANKS[n][0], FILTER_BANKS[n][1], on_scalar=(u == 0 or b == 0))
+                    if b + 1 < IMAGES and n < len(FILTER_STEPS):
+                        for window, filters in FILTER_STEPS[n]:
+                            filter_bank(b + 1, window, filters, on_scalar=(u == 0 or b == 0))
                 behind = b * HIDDEN_PASSES + g - LAG
                 if behind >= 0:
                     second_layer(behind // HIDDEN_PASSES, behind % HIDDEN_PASSES)
@@ -295,7 +320,8 @@ def tile_nn_kernel(tc, state_grid, w_hidden_words, w_hidden_scales, w_out_words,
                 if b == 0 and g + 2 < HIDDEN_PASSES:
                     sort_hidden_units(g + 2)
                 if b + 2 < IMAGES and g == 2:
-                    sort_channels(b + 2, on_scalar=True)
+                    for w in range(WINDOWS):
+                        sort_channels(b + 2, w, "gpsimd")
                 if b + 1 < IMAGES and g > 0:
                     quantise_perception(b + 1, PASS_ORDER[g - 1])
                 quantise_hidden(b, g)

@@ -24,6 +24,7 @@ WINDOW_ROWS = P // SIDE
 INNER_ROWS = WINDOW_ROWS - 2
 WINDOWS = 3
 TOGETHER = 2
+FIRST_ROW = (1, 1, 0, 0)
 FILTERS = 3
 HIDDEN_PASSES = HIDDEN // K_PASS
 PAIR = 2
@@ -70,7 +71,7 @@ def tile_nn_kernel(tc, state_grid, w_hidden_words, w_hidden_scales, w_out_words,
                 "(b q) c -> q b c", b=TOGETHER
             )
             for w in range(WINDOWS):
-                first = INNER_ROWS * w * SIDE
+                first = (FIRST_ROW[first_image] - 1 + INNER_ROWS * w) % SIDE * SIDE
                 inside = min(P, IMAGE - first)
                 nc.sync.dma_start(out=raw[:inside, :, w, :], in_=rows[first : first + inside])
                 if inside < P:
@@ -268,17 +269,17 @@ def tile_nn_kernel(tc, state_grid, w_hidden_words, w_hidden_scales, w_out_words,
                     stop=(g == HIDDEN_PASSES - 1),
                 )
 
-        def store(b, half, on_scalar):
+        def store(b, half, on_scalar, queue):
             result = work.tile([P, CHANNELS], F32, name="result%d_%d" % (b, half), tag="result", bufs=4)
             if on_scalar:
                 nc.scalar.copy(out=result[:], in_=out_sums[b, half][:])
             else:
                 nc.vector.tensor_copy(out=result[:], in_=out_sums[b, half][:])
-            first = b * IMAGE + half * P + SIDE
-            inside = min(P, (b + 1) * IMAGE - first)
-            nc.sync.dma_start(out=out_rows[first : first + inside, :], in_=result[:inside, :])
+            first = half * P + FIRST_ROW[b] * SIDE
+            inside = min(P, IMAGE - first)
+            queue.dma_start(out=out_rows[b * IMAGE + first : b * IMAGE + first + inside, :], in_=result[:inside, :])
             if inside < P:
-                nc.sync.dma_start(out=out_rows[b * IMAGE : b * IMAGE + P - inside, :], in_=result[inside:, :])
+                queue.dma_start(out=out_rows[b * IMAGE : b * IMAGE + P - inside, :], in_=result[inside:, :])
 
         sort_channels(0, 0, "scalar")
         sort_channels(0, 1, "scalar")
@@ -315,8 +316,8 @@ def tile_nn_kernel(tc, state_grid, w_hidden_words, w_hidden_scales, w_out_words,
                 if behind >= 0:
                     second_layer(behind // HIDDEN_PASSES, behind % HIDDEN_PASSES)
                     if behind % HIDDEN_PASSES == HIDDEN_PASSES - 1:
-                        store(behind // HIDDEN_PASSES, 0, on_scalar=True)
-                        store(behind // HIDDEN_PASSES, 1, on_scalar=True)
+                        store(behind // HIDDEN_PASSES, 0, on_scalar=True, queue=nc.sync)
+                        store(behind // HIDDEN_PASSES, 1, on_scalar=True, queue=nc.sync)
                 if b == 0 and g + 2 < HIDDEN_PASSES:
                     sort_hidden_units(g + 2)
                 if b + 2 < IMAGES and g == 2:
@@ -327,5 +328,5 @@ def tile_nn_kernel(tc, state_grid, w_hidden_words, w_hidden_scales, w_out_words,
                 quantise_hidden(b, g)
         for g in range(HIDDEN_PASSES - LAG, HIDDEN_PASSES):
             second_layer(IMAGES - 1, g)
-        store(IMAGES - 1, 0, on_scalar=True)
-        store(IMAGES - 1, 1, on_scalar=False)
+        store(IMAGES - 1, 0, on_scalar=True, queue=nc.scalar)
+        store(IMAGES - 1, 1, on_scalar=False, queue=nc.sync)

@@ -88,7 +88,6 @@ def tile_nn_kernel(tc, state_grid, w_hidden_words, w_hidden_scales, w_out_words,
                 )
 
         load_images(0)
-        load_planes(wh_planes_raw, w_hidden_scales)
         wh_bytes = w_hidden_words.rearrange("f p n t -> p f (n t)")
         wh_raw = []
         for g in range(HIDDEN_PASSES):
@@ -98,13 +97,15 @@ def tile_nn_kernel(tc, state_grid, w_hidden_words, w_hidden_scales, w_out_words,
                 in_=wh_bytes[:, :, g * BANK * PACK : (g + 1) * BANK * PACK].bitcast(I32),
             )
             wh_raw.append(block)
+            if g == 0:
+                load_planes(wh_planes_raw, w_hidden_scales)
         load_planes(wo_planes, w_out_scales)
         wo_words = keep.tile([P, HIDDEN_PASSES, CHANNELS], U32, align_bytes=64)
-        nc.sync.dma_start(
-            out=wo_words[:].bitcast(I32),
-            in_=w_out_words.rearrange("g p n t -> p g (n t)").bitcast(I32),
-        )
+        wo_bytes = w_out_words.rearrange("g p n t -> p g (n t)")
+        early = HIDDEN_PASSES // 2
+        nc.sync.dma_start(out=wo_words[:, :early, :].bitcast(I32), in_=wo_bytes[:, :early, :].bitcast(I32))
         load_images(TOGETHER)
+        nc.sync.dma_start(out=wo_words[:, early:, :].bitcast(I32), in_=wo_bytes[:, early:, :].bitcast(I32))
 
         ident_bf16 = keep.tile([P, P], BF16)
         make_identity(nc, ident_bf16[:])

@@ -142,7 +142,6 @@ def tile_nn_kernel(tc, state_grid, w_hidden_words, w_hidden_scales, w_out_words,
 
         wh_planes = keep.tile([P, HIDDEN], U8, align_bytes=64)
         wh_words = {}
-        sorted_state = {}
         perception = {}
         perception_words = {}
         perception_scales = {}
@@ -165,20 +164,6 @@ def tile_nn_kernel(tc, state_grid, w_hidden_words, w_hidden_scales, w_out_words,
                 )
             wh_words[g] = by_t
 
-        def sort_channels(b, w, engine):
-            if b not in sorted_state:
-                sorted_state[b] = keep.tile([P, WINDOWS, PACK, P], BF16, name="sorted%d" % b)
-            together = sorted_state[b][:, w].rearrange("q t (c i) -> q c t i", i=2 * LINE)
-            as_loaded = state[b][:, w, :].rearrange("q (c i t) -> q c t i", i=2 * LINE, t=PACK)
-            if engine == "scalar":
-                nc.scalar.copy(out=together, in_=as_loaded)
-            elif engine == "vector":
-                nc.vector.tensor_copy(out=together, in_=as_loaded)
-            else:
-                nc.gpsimd.tensor_scalar(
-                    out=together, in0=as_loaded, scalar1=1.0, scalar2=0.0, op0=ALU.mult, op1=ALU.add
-                )
-
         def filter_bank(b, w, filters, on_scalar):
             if b not in perception:
                 perception[b] = work.tile(
@@ -190,7 +175,7 @@ def tile_nn_kernel(tc, state_grid, w_hidden_words, w_hidden_scales, w_out_words,
             for t in range(PACK):
                 nc.tensor.matmul(
                     out=bank[:, t],
-                    lhsT=sorted_state[b][:, w, t, :],
+                    lhsT=state[b][:, w, :].rearrange("q (p t) -> q t p", t=PACK)[:, t, :],
                     rhs=(ident_bf16[:, SIDE : SIDE + width] if filters[0] == FILTERS - 1 else taps[:, filters[0] : filters[-1] + 1, :width]),
                     start=True,
                     stop=True,
@@ -282,11 +267,6 @@ def tile_nn_kernel(tc, state_grid, w_hidden_words, w_hidden_scales, w_out_words,
             if inside < P:
                 queue.dma_start(out=out_rows[b * IMAGE : b * IMAGE + P - inside, :], in_=result[inside:, :])
 
-        sort_channels(0, 0, "scalar")
-        sort_channels(0, 1, "scalar")
-        sort_channels(0, 2, "vector")
-        for w in range(WINDOWS):
-            sort_channels(1, w, "gpsimd")
         filter_bank(0, 0, (2,), on_scalar=True)
         filter_bank(0, 1, (2,), on_scalar=False)
         filter_bank(0, 2, (2,), on_scalar=True)
@@ -321,9 +301,6 @@ def tile_nn_kernel(tc, state_grid, w_hidden_words, w_hidden_scales, w_out_words,
                         store(behind // HIDDEN_PASSES, 1, on_scalar=True, queue=nc.sync)
                 if b == 0 and g + 2 < HIDDEN_PASSES:
                     sort_hidden_units(g + 2)
-                if b + 2 < IMAGES and g == 2:
-                    for w in range(WINDOWS):
-                        sort_channels(b + 2, w, "gpsimd")
                 if b + 1 < IMAGES and g > 0:
                     quantise_perception(b + 1, PASS_ORDER[g - 1])
                 quantise_hidden(b, g)

@@ -39,6 +39,15 @@ FILTER_STEPS = [
     [(0, (1,))],
     [(1, (1,))],
 ]
+SOBEL_STEPS = [
+    [(0, (0,)), (1, (0,))],
+    [(2, (0, 1))],
+    [(0, (1,))],
+    [(1, (1,))],
+]
+SQUARE = 32
+BLOCKS = IMAGE // SQUARE
+QUARTER = CHANNELS // 4
 PASS_ORDER = (2, 0, 1)
 HEAD_FILL = 6
 LAG = 3
@@ -105,6 +114,15 @@ def tile_nn_kernel(tc, state_grid, w_hidden_words, w_hidden_scales, w_out_words,
         early = HIDDEN_PASSES // 2
         nc.sync.dma_start(out=wo_words[:, :early, :].bitcast(I32), in_=wo_bytes[:, :early, :].bitcast(I32))
         load_images(TOGETHER)
+        square_raw = keep.tile([P, TOGETHER, BLOCKS, QUARTER], BF16, align_bytes=64)
+        last_rows = state_rows[TOGETHER * IMAGE :, :]
+        for quadrant in range(4):
+            nc.sync.dma_start(
+                out=square_raw[SQUARE * quadrant : SQUARE * (quadrant + 1)].rearrange("p i k c -> p (i k) c"),
+                in_=last_rows[:, quadrant * QUARTER : (quadrant + 1) * QUARTER].rearrange(
+                    "(k p) c -> p k c", p=SQUARE
+                ),
+            )
         nc.sync.dma_start(out=wo_words[:, early:, :].bitcast(I32), in_=wo_bytes[:, early:, :].bitcast(I32))
 
         ident_bf16 = keep.tile([P, P], BF16)
@@ -165,13 +183,9 @@ def tile_nn_kernel(tc, state_grid, w_hidden_words, w_hidden_scales, w_out_words,
             wh_words[g] = by_t
 
         def filter_bank(b, w, filters, on_scalar):
-            if b not in perception:
-                perception[b] = work.tile(
-                    [P, FILTERS, IMAGE, PACK], BF16, name="perception%d" % b, tag="perception", align_bytes=64
-                )
             first = INNER_ROWS * w * SIDE
             width = min(INNER_ROWS * SIDE, IMAGE - first)
-            bank = banks.tile([P, PACK, len(filters), width], F32, tag="bank")
+            bank = banks.tile([P, PACK, len(filters), width], BF16, tag="bank")
             for t in range(PACK):
                 nc.tensor.matmul(
                     out=bank[:, t],
@@ -181,11 +195,43 @@ def tile_nn_kernel(tc, state_grid, w_hidden_words, w_hidden_scales, w_out_words,
                     stop=True,
                 )
             side_by_side = bank[:].rearrange("p t f q -> p f q t")
-            place = perception[b][:, filters[0] : filters[-1] + 1, first : first + width, :]
+            place = perception_tile(b)[:, filters[0] : filters[-1] + 1, first : first + width, :]
             if on_scalar:
                 nc.scalar.copy(out=place, in_=side_by_side)
             else:
                 nc.vector.tensor_copy(out=place, in_=side_by_side)
+
+        squares = {}
+
+        def perception_tile(b):
+            if b not in perception:
+                perception[b] = work.tile(
+                    [P, FILTERS, IMAGE, PACK], BF16, name="perception%d" % b, tag="perception", align_bytes=64
+                )
+            return perception[b]
+
+        def sort_words(b):
+            squares[b] = work.tile([P, BLOCKS, 2, SQUARE], I32, name="by_word%d" % b, tag="by_word", align_bytes=64)
+            nc.vector.tensor_copy(
+                out=squares[b][:],
+                in_=square_raw[:, b - TOGETHER].bitcast(I32).rearrange("p k (r v) -> p k v r", v=2),
+            )
+
+        def turn_squares(b):
+            turned = work.tile([P, BLOCKS, 2, SQUARE], I32, name="turned%d" % b, tag="turned", align_bytes=64)
+            nc.vector.transpose(
+                out=turned[:].rearrange("p k v q -> p (k v q)").bitcast(F32),
+                in_=squares[b][:].rearrange("p k v q -> p (k v q)").bitcast(F32),
+            )
+            squares[b] = turned
+
+        def lay_state(b):
+            nc.vector.tensor_copy(
+                out=perception_tile(b)[:, FILTERS - 1].rearrange("p q t -> p (q t)").bitcast(I32).rearrange(
+                    "p (k q v) -> p k q v", k=BLOCKS, v=2
+                ),
+                in_=squares[b][:].rearrange("p k v q -> p k q v"),
+            )
 
         def quantise_perception(b, f):
             if b not in perception_words:
@@ -289,10 +335,11 @@ def tile_nn_kernel(tc, state_grid, w_hidden_words, w_hidden_scales, w_out_words,
                 for u in range(PAIR):
                     step = PAIR * g + u
                     first_layer(b, g, u)
-                    n = step + (HEAD_FILL if b == 0 else 0)
-                    if b + 1 < IMAGES and n < len(FILTER_STEPS):
-                        for window, filters in FILTER_STEPS[n]:
-                            filter_bank(b + 1, window, filters, on_scalar=(u == 0 or b == 0))
+                    if 0 < b < IMAGES - 1 and step < len(SOBEL_STEPS):
+                        for window, filters in SOBEL_STEPS[step]:
+                            filter_bank(b + 1, window, filters, on_scalar=(u == 0))
+                    if 0 < b < IMAGES - 1 and step < 3:
+                        (sort_words, turn_squares, lay_state)[step](b + 1)
                 behind = b * HIDDEN_PASSES + g - LAG
                 if behind >= 0:
                     second_layer(behind // HIDDEN_PASSES, behind % HIDDEN_PASSES)

@@ -26,31 +26,17 @@ WINDOWS = 3
 TOGETHER = 2
 FIRST_ROW = (1, 1, 0, 0)
 FILTERS = 3
+SOBELS = 2
+STATE = 2
+PASS_ORDER = (2, 0, 1)
 HIDDEN_PASSES = HIDDEN // K_PASS
 PAIR = 2
 LINE = 4
 PADDED = SIDE + 2
-
-FILTER_STEPS = [
-    [(0, (2,)), (1, (2,))],
-    [(2, (2,))],
-    [(0, (0,)), (1, (0,))],
-    [(2, (0, 1))],
-    [(0, (1,))],
-    [(1, (1,))],
-]
-SOBEL_STEPS = [
-    [(0, (0,)), (1, (0,))],
-    [(2, (0, 1))],
-    [(0, (1,))],
-    [(1, (1,))],
-]
 SQUARE = 32
 BLOCKS = IMAGE // SQUARE
 QUARTER = CHANNELS // 4
-PASS_ORDER = (2, 0, 1)
-HEAD_FILL = 6
-LAG = 3
+WARM_UP = 3
 
 FLOPS = 2 * IMAGES * IMAGE * (FILTERS * CHANNELS * HIDDEN + HIDDEN * CHANNELS)
 
@@ -69,7 +55,9 @@ def tile_nn_kernel(tc, state_grid, w_hidden_words, w_hidden_scales, w_out_words,
 
         wh_planes_raw = keep.tile([P, HIDDEN], U8, align_bytes=64)
         wo_planes = keep.tile([P, CHANNELS], U8, align_bytes=64)
+        nothing = keep.tile([P, BANK], BF16)
         nc.vector.memset(wh_planes_raw[:].bitcast(I32), 0)
+        nc.vector.memset(nothing[:], 0.0)
         nc.vector.memset(wo_planes[:].bitcast(I32), 0)
 
         state = {}
@@ -96,44 +84,53 @@ def tile_nn_kernel(tc, state_grid, w_hidden_words, w_hidden_scales, w_out_words,
                     in_=scales[:, 4 * quadrant : 4 * quadrant + 4, :].bitcast(I32),
                 )
 
-        load_images(0)
         wh_bytes = w_hidden_words.rearrange("f p n t -> p f (n t)")
         wh_raw = []
-        for g in range(HIDDEN_PASSES):
+
+        def load_block(g):
             block = keep.tile([P, FILTERS, BANK], U32, name="wh_raw%d" % g, align_bytes=64)
             nc.sync.dma_start(
                 out=block[:].bitcast(I32),
                 in_=wh_bytes[:, :, g * BANK * PACK : (g + 1) * BANK * PACK].bitcast(I32),
             )
             wh_raw.append(block)
-            if g == 0:
-                load_planes(wh_planes_raw, w_hidden_scales)
+
+        load_images(0)
+        load_block(0)
+        load_planes(wh_planes_raw, w_hidden_scales)
+        load_block(1)
+        load_block(2)
+        load_block(3)
+        load_images(TOGETHER)
         load_planes(wo_planes, w_out_scales)
         wo_words = keep.tile([P, HIDDEN_PASSES, CHANNELS], U32, align_bytes=64)
-        wo_bytes = w_out_words.rearrange("g p n t -> p g (n t)")
-        early = HIDDEN_PASSES // 2
-        nc.sync.dma_start(out=wo_words[:, :early, :].bitcast(I32), in_=wo_bytes[:, :early, :].bitcast(I32))
-        load_images(TOGETHER)
-        square_raw = keep.tile([P, TOGETHER, BLOCKS, QUARTER], BF16, align_bytes=64)
-        last_rows = state_rows[TOGETHER * IMAGE :, :]
-        for quadrant in range(4):
-            nc.sync.dma_start(
-                out=square_raw[SQUARE * quadrant : SQUARE * (quadrant + 1)].rearrange("p i k c -> p (i k) c"),
-                in_=last_rows[:, quadrant * QUARTER : (quadrant + 1) * QUARTER].rearrange(
-                    "(k p) c -> p k c", p=SQUARE
-                ),
-            )
-        nc.sync.dma_start(out=wo_words[:, early:, :].bitcast(I32), in_=wo_bytes[:, early:, :].bitcast(I32))
+        nc.sync.dma_start(
+            out=wo_words[:].bitcast(I32), in_=w_out_words.rearrange("g p n t -> p g (n t)").bitcast(I32)
+        )
+        square_raw = [
+            keep.tile([P, BLOCKS, QUARTER], BF16, name="square_raw%d" % b, align_bytes=64) for b in range(TOGETHER)
+        ]
+        for b in range(TOGETHER):
+            rows = state_rows[(TOGETHER + b) * IMAGE : (TOGETHER + b + 1) * IMAGE, :]
+            for quadrant in range(4):
+                nc.sync.dma_start(
+                    out=square_raw[b][SQUARE * quadrant : SQUARE * (quadrant + 1)],
+                    in_=rows[:, quadrant * QUARTER : (quadrant + 1) * QUARTER].rearrange("(k p) c -> p k c", p=SQUARE),
+                )
 
         ident_bf16 = keep.tile([P, P], BF16)
         make_identity(nc, ident_bf16[:])
+
+        idle = sums.tile([P, BANK], F32, name="idle", tag="sums")
+        for n in range(WARM_UP):
+            nc.tensor.matmul(out=idle[:], lhsT=nothing[:, :P], rhs=nothing[:], start=True, stop=True)
 
         padded = keep.tile([P, WINDOW_ROWS, PADDED], BF16)
         nc.vector.tensor_copy(out=padded[:, :, 1 : 1 + SIDE], in_=ident_bf16[:].rearrange("k (a c) -> k a c", c=SIDE))
         nc.vector.tensor_copy(out=padded[:, :, 0:1], in_=padded[:, :, SIDE : SIDE + 1])
         nc.vector.tensor_copy(out=padded[:, :, SIDE + 1 :], in_=padded[:, :, 1:2])
 
-        taps = keep.tile([P, FILTERS - 1, INNER_ROWS * SIDE], BF16)
+        taps = keep.tile([P, SOBELS, INNER_ROWS * SIDE], BF16)
         diff_x = keep.tile([P, WINDOW_ROWS, SIDE], BF16)
         part_x = keep.tile([P, INNER_ROWS, SIDE], BF16)
         part_y = keep.tile([P, WINDOW_ROWS, SIDE], BF16)
@@ -160,61 +157,93 @@ def tile_nn_kernel(tc, state_grid, w_hidden_words, w_hidden_scales, w_out_words,
 
         wh_planes = keep.tile([P, HIDDEN], U8, align_bytes=64)
         wh_words = {}
-        perception = {}
-        perception_words = {}
-        perception_scales = {}
-        hidden = {}
-        hidden_words = {}
-        hidden_scales = {}
+        state_banks = {}
+        squares = {}
         out_sums = {}
+        perception = [
+            keep.tile([P, FILTERS, IMAGE, PACK], BF16, name="perception%d" % b, align_bytes=64) for b in range(IMAGES)
+        ]
+        perception_words = [
+            keep.tile([P, FILTERS, IMAGE], U32, name="perception_words%d" % b, align_bytes=64) for b in range(IMAGES)
+        ]
+        perception_scales = [
+            keep.tile([P, FILTERS, IMAGE], U8, name="perception_scales%d" % b, align_bytes=64) for b in range(IMAGES)
+        ]
+        hidden = [
+            keep.tile([P, HIDDEN_PASSES, IMAGE, PACK], BF16, name="hidden%d" % b, align_bytes=64) for b in range(IMAGES)
+        ]
+        hidden_words = [
+            keep.tile([P, HIDDEN_PASSES, IMAGE], U32, name="hidden_words%d" % b, align_bytes=64) for b in range(IMAGES)
+        ]
+        hidden_scales = [
+            keep.tile([P, HIDDEN_PASSES, IMAGE], U8, name="hidden_scales%d" % b, align_bytes=64) for b in range(IMAGES)
+        ]
 
-        def sort_hidden_units(g):
+        def sort_planes(g):
             columns = slice(g * BANK, (g + 1) * BANK)
             nc.vector.tensor_copy(
                 out=wh_planes[:, columns].rearrange("r (t m) -> r t m", t=PACK),
                 in_=wh_planes_raw[:, columns].rearrange("r (m t) -> r t m", t=PACK),
             )
-            by_t = keep.tile([P, FILTERS, PACK, P], U32, name="wh_words%d" % g, align_bytes=64)
-            for f in PASS_ORDER:
-                nc.vector.tensor_copy(
-                    out=by_t[:, f].bitcast(I32).rearrange("k t (c i) -> k c t i", i=LINE),
-                    in_=wh_raw[g][:, f, :].bitcast(I32).rearrange("k (c i t) -> k c t i", i=LINE, t=PACK),
-                )
-            wh_words[g] = by_t
 
-        def filter_bank(b, w, filters, on_scalar):
+        def sort_block(g, f, engine=None):
+            if g not in wh_words:
+                wh_words[g] = keep.tile([P, FILTERS, PACK, P], U32, name="wh_words%d" % g, align_bytes=64)
+            (engine or nc.vector).tensor_copy(
+                out=wh_words[g][:, f].bitcast(I32).rearrange("k t (c i) -> k c t i", i=LINE),
+                in_=wh_raw[g][:, f, :].bitcast(I32).rearrange("k (c i t) -> k c t i", i=LINE, t=PACK),
+            )
+
+        def sort_hidden_units(g):
+            sort_planes(g)
+            for f in PASS_ORDER:
+                sort_block(g, f)
+
+        def inner(w):
             first = INNER_ROWS * w * SIDE
-            width = min(INNER_ROWS * SIDE, IMAGE - first)
-            bank = banks.tile([P, PACK, len(filters), width], BF16, tag="bank")
+            return first, min(INNER_ROWS * SIDE, IMAGE - first)
+
+        def channels_of(b, w, t):
+            return state[b][:, w, :].rearrange("q (p t) -> q t p", t=PACK)[:, t, :]
+
+        def copy_out(place, bank, on_scalar):
+            if on_scalar:
+                nc.scalar.copy(out=place, in_=bank)
+            else:
+                nc.vector.tensor_copy(out=place, in_=bank)
+
+        def state_window(b, w):
+            if w == 0:
+                state_banks[b] = banks.tile([P, PACK, IMAGE], BF16, name="state_bank%d" % b, tag="bank")
+            first, width = inner(w)
             for t in range(PACK):
                 nc.tensor.matmul(
-                    out=bank[:, t],
-                    lhsT=state[b][:, w, :].rearrange("q (p t) -> q t p", t=PACK)[:, t, :],
-                    rhs=(ident_bf16[:, SIDE : SIDE + width] if filters[0] == FILTERS - 1 else taps[:, filters[0] : filters[-1] + 1, :width]),
+                    out=state_banks[b][:, t, first : first + width],
+                    lhsT=channels_of(b, w, t),
+                    rhs=ident_bf16[:, SIDE : SIDE + width],
                     start=True,
                     stop=True,
                 )
-            side_by_side = bank[:].rearrange("p t f q -> p f q t")
-            place = perception_tile(b)[:, filters[0] : filters[-1] + 1, first : first + width, :]
-            if on_scalar:
-                nc.scalar.copy(out=place, in_=side_by_side)
-            else:
-                nc.vector.tensor_copy(out=place, in_=side_by_side)
 
-        squares = {}
+        def state_out(b, on_scalar):
+            copy_out(perception[b][:, STATE], state_banks[b][:].rearrange("p t q -> p q t"), on_scalar)
 
-        def perception_tile(b):
-            if b not in perception:
-                perception[b] = work.tile(
-                    [P, FILTERS, IMAGE, PACK], BF16, name="perception%d" % b, tag="perception", align_bytes=64
+        def sobel_window(b, w, on_scalar):
+            first, width = inner(w)
+            bank = banks.tile([P, PACK, SOBELS, width], BF16, tag="bank")
+            for t in range(PACK):
+                nc.tensor.matmul(
+                    out=bank[:, t], lhsT=channels_of(b, w, t), rhs=taps[:, :, :width], start=True, stop=True
                 )
-            return perception[b]
+            copy_out(
+                perception[b][:, :SOBELS, first : first + width, :], bank[:].rearrange("p t f q -> p f q t"), on_scalar
+            )
 
         def sort_words(b):
             squares[b] = work.tile([P, BLOCKS, 2, SQUARE], I32, name="by_word%d" % b, tag="by_word", align_bytes=64)
             nc.vector.tensor_copy(
                 out=squares[b][:],
-                in_=square_raw[:, b - TOGETHER].bitcast(I32).rearrange("p k (r v) -> p k v r", v=2),
+                in_=square_raw[b - TOGETHER][:].bitcast(I32).rearrange("p k (r v) -> p k v r", v=2),
             )
 
         def turn_squares(b):
@@ -227,31 +256,20 @@ def tile_nn_kernel(tc, state_grid, w_hidden_words, w_hidden_scales, w_out_words,
 
         def lay_state(b):
             nc.vector.tensor_copy(
-                out=perception_tile(b)[:, FILTERS - 1].rearrange("p q t -> p (q t)").bitcast(I32).rearrange(
+                out=perception[b][:, STATE].rearrange("p q t -> p (q t)").bitcast(I32).rearrange(
                     "p (k q v) -> p k q v", k=BLOCKS, v=2
                 ),
                 in_=squares[b][:].rearrange("p k v q -> p k q v"),
             )
 
-        def quantise_perception(b, f):
-            if b not in perception_words:
-                perception_words[b] = keep.tile(
-                    [P, FILTERS, IMAGE], U32, name="perception_words%d" % b, align_bytes=64
-                )
-                perception_scales[b] = keep.tile(
-                    [P, FILTERS, IMAGE], U8, name="perception_scales%d" % b, align_bytes=64
-                )
+        def quantise_perception(b, filters):
             nc.vector.quantize_mx(
-                out=perception_words[b][:, f, :].bitcast(FP8X4),
-                scales=perception_scales[b][:, f, :],
-                in_=perception[b][:, f].rearrange("p q t -> p (q t)"),
+                out=perception_words[b][:, filters, :].rearrange("p f q -> p (f q)").bitcast(FP8X4),
+                scales=perception_scales[b][:, filters, :].rearrange("p f q -> p (f q)"),
+                in_=perception[b][:, filters].rearrange("p f q t -> p (f q t)"),
             )
 
-        def first_layer(b, g, u):
-            if b not in hidden:
-                hidden[b] = work.tile(
-                    [P, HIDDEN_PASSES, IMAGE, PACK], BF16, name="hidden%d" % b, tag="hidden", align_bytes=64
-                )
+        def first_layer(b, g, u, on_scalar):
             bank = banks.tile([P, PAIR, IMAGE], F32, tag="bank")
             for e in range(PAIR):
                 t = PAIR * u + e
@@ -268,19 +286,12 @@ def tile_nn_kernel(tc, state_grid, w_hidden_words, w_hidden_scales, w_out_words,
                     )
             place = hidden[b][:, g, :, PAIR * u : PAIR * (u + 1)]
             side_by_side = bank[:].rearrange("p e q -> p q e")
-            if u == 0 and b > 0:
-                nc.vector.tensor_scalar_max(out=place, in0=side_by_side, scalar1=0.0)
-            else:
+            if on_scalar:
                 nc.scalar.activation(out=place, in_=side_by_side, func=RELU)
+            else:
+                nc.vector.tensor_scalar_max(out=place, in0=side_by_side, scalar1=0.0)
 
         def quantise_hidden(b, g):
-            if b not in hidden_words:
-                hidden_words[b] = work.tile(
-                    [P, HIDDEN_PASSES, IMAGE], U32, name="hidden_words%d" % b, tag="hidden_words", align_bytes=64
-                )
-                hidden_scales[b] = work.tile(
-                    [P, HIDDEN_PASSES, IMAGE], U8, name="hidden_scales%d" % b, tag="hidden_scales", align_bytes=64
-                )
             nc.vector.quantize_mx(
                 out=hidden_words[b][:, g, :].bitcast(FP8X4),
                 scales=hidden_scales[b][:, g, :],
@@ -303,55 +314,49 @@ def tile_nn_kernel(tc, state_grid, w_hidden_words, w_hidden_scales, w_out_words,
 
         def store(b, half, on_scalar, queue):
             result = work.tile([P, CHANNELS], F32, name="result%d_%d" % (b, half), tag="result", bufs=4)
-            if on_scalar:
-                nc.scalar.copy(out=result[:], in_=out_sums[b, half][:])
-            else:
-                nc.vector.tensor_copy(out=result[:], in_=out_sums[b, half][:])
+            copy_out(result[:], out_sums[b, half][:], on_scalar)
             first = half * P + FIRST_ROW[b] * SIDE
             inside = min(P, IMAGE - first)
             queue.dma_start(out=out_rows[b * IMAGE + first : b * IMAGE + first + inside, :], in_=result[:inside, :])
             if inside < P:
                 queue.dma_start(out=out_rows[b * IMAGE : b * IMAGE + P - inside, :], in_=result[inside:, :])
 
-        filter_bank(0, 0, (2,), on_scalar=True)
-        filter_bank(0, 1, (2,), on_scalar=False)
-        filter_bank(0, 2, (2,), on_scalar=True)
-        filter_bank(0, 0, (0,), on_scalar=False)
-        quantise_perception(0, 2)
-        filter_bank(0, 1, (0,), on_scalar=True)
-        filter_bank(0, 2, (0, 1), on_scalar=False)
-        filter_bank(0, 0, (1,), on_scalar=False)
-        filter_bank(0, 1, (1,), on_scalar=True)
-        quantise_perception(0, 0)
-        quantise_perception(0, 1)
-        for n in range(HEAD_FILL):
-            for window, filters in FILTER_STEPS[n]:
-                filter_bank(1, window, filters, on_scalar=True)
-        sort_hidden_units(0)
-        sort_hidden_units(1)
+        STATE_ONLY = slice(STATE, FILTERS)
+        BOTH_SOBELS = slice(0, SOBELS)
+        for w in range(WINDOWS):
+            state_window(0, w)
+            if w == WINDOWS - 1:
+                state_out(0, on_scalar=True)
+            sobel_window(0, w, on_scalar=(w == 0))
+        quantise_perception(0, BOTH_SOBELS)
+        quantise_perception(0, STATE_ONLY)
+        for w in range(WINDOWS):
+            state_window(1, w)
+            if w == WINDOWS - 1:
+                state_out(1, on_scalar=True)
+            sobel_window(1, w, on_scalar=True)
+        sort_block(0, 2)
+        sort_planes(0)
+        sort_block(0, 0)
+        sort_block(0, 1)
+        quantise_perception(1, BOTH_SOBELS)
+        quantise_perception(1, STATE_ONLY)
 
-        for b in range(IMAGES):
-            for g in range(HIDDEN_PASSES):
-                for u in range(PAIR):
-                    step = PAIR * g + u
-                    first_layer(b, g, u)
-                    if 0 < b < IMAGES - 1 and step < len(SOBEL_STEPS):
-                        for window, filters in SOBEL_STEPS[step]:
-                            filter_bank(b + 1, window, filters, on_scalar=(u == 0))
-                    if 0 < b < IMAGES - 1 and step < 3:
-                        (sort_words, turn_squares, lay_state)[step](b + 1)
-                behind = b * HIDDEN_PASSES + g - LAG
-                if behind >= 0:
-                    second_layer(behind // HIDDEN_PASSES, behind % HIDDEN_PASSES)
-                    if behind % HIDDEN_PASSES == HIDDEN_PASSES - 1:
-                        store(behind // HIDDEN_PASSES, 0, on_scalar=True, queue=nc.sync)
-                        store(behind // HIDDEN_PASSES, 1, on_scalar=True, queue=nc.sync)
-                if b == 0 and g + 2 < HIDDEN_PASSES:
-                    sort_hidden_units(g + 2)
-                if b + 1 < IMAGES and g > 0:
-                    quantise_perception(b + 1, PASS_ORDER[g - 1])
-                quantise_hidden(b, g)
-        for g in range(HIDDEN_PASSES - LAG, HIDDEN_PASSES):
-            second_layer(IMAGES - 1, g)
-        store(IMAGES - 1, 0, on_scalar=True, queue=nc.scalar)
-        store(IMAGES - 1, 1, on_scalar=False, queue=nc.sync)
+        slots = [(0, 0), (1, 0), (0, 1), (1, 1), (0, 2), (0, 3), (1, 2), (1, 3)]
+        slots += [(b, g) for b in range(2, IMAGES) for g in range(HIDDEN_PASSES)]
+        tensor_extras = {(5,0): [(sobel_window, 2, 0, True)], (5,1): [(sobel_window, 2, 1, True)], (6,0): [(sobel_window, 2, 2, True), (second_layer, 0, 0)], (6,1): [(second_layer, 0, 1)], (7,0): [(second_layer, 0, 2)], (7,1): [(second_layer, 0, 3), (store, 0, 0, True, nc.sync), (store, 0, 1, False, nc.sync)], (9,0): [(second_layer, 1, 0), (sobel_window, 3, 2, True)], (9,1): [(second_layer, 1, 1)], (10,0): [(second_layer, 1, 2)], (10,1): [(second_layer, 1, 3), (store, 1, 0, True, nc.sync), (store, 1, 1, False, nc.sync)], (8,0): [(sobel_window, 3, 0, True)], (8,1): [(sobel_window, 3, 1, True)], (13,0): [(second_layer, 2, 0)], (13,1): [(second_layer, 2, 1)], (14,0): [(second_layer, 2, 2)], (14,1): [(second_layer, 2, 3), (store, 2, 0, True, nc.sync), (store, 2, 1, False, nc.sync)]}
+        vector_extras = {0: [(sort_hidden_units, 1)], 2: [(sort_hidden_units, 2)], 3: [(sort_hidden_units, 3)], 5: [(sort_words, 2)], 6: [(turn_squares, 2), (lay_state, 2), (quantise_perception, 2, STATE_ONLY), (quantise_perception, 2, BOTH_SOBELS)], 8: [(sort_words, 3)], 9: [(turn_squares, 3), (lay_state, 3)], 10: [(quantise_perception, 3, STATE_ONLY), (quantise_perception, 3, BOTH_SOBELS)]}
+        for k, (b, g) in enumerate(slots):
+            for u in range(PAIR):
+                first_layer(b, g, u, on_scalar=(u == 1 or k in (2, 3, 4)))
+                for call, *args in tensor_extras.get((k, u), ()):
+                    call(*args)
+            for call, *args in vector_extras.get(k, ()):
+                call(*args)
+            if k > 0:
+                quantise_hidden(*slots[k - 1])
+        quantise_hidden(3, HIDDEN_PASSES - 1)
+        for g in range(0, HIDDEN_PASSES):
+            second_layer(3, g)
+        store(3, 0, on_scalar=True, queue=nc.scalar)
+        store(3, 1, on_scalar=False, queue=nc.sync)

@@ -36,7 +36,7 @@ PADDED = SIDE + 2
 SQUARE = 32
 BLOCKS = IMAGE // SQUARE
 QUARTER = CHANNELS // 4
-WARM_UP = 3
+WARM_UP = 14
 
 FLOPS = 2 * IMAGES * IMAGE * (FILTERS * CHANNELS * HIDDEN + HIDDEN * CHANNELS)
 
@@ -55,9 +55,10 @@ def tile_nn_kernel(tc, state_grid, w_hidden_words, w_hidden_scales, w_out_words,
 
         wh_planes_raw = keep.tile([P, HIDDEN], U8, align_bytes=64)
         wo_planes = keep.tile([P, CHANNELS], U8, align_bytes=64)
-        nothing = keep.tile([P, BANK], BF16)
-        nc.vector.memset(wh_planes_raw[:].bitcast(I32), 0)
+        nothing = keep.tile([P, P], BF16)
         nc.vector.memset(nothing[:], 0.0)
+        nc.scalar.activation(out=keep.tile([P, P], BF16, name="table")[:], in_=nothing[:], func=RELU)
+        nc.vector.memset(wh_planes_raw[:].bitcast(I32), 0)
         nc.vector.memset(wo_planes[:].bitcast(I32), 0)
 
         state = {}
@@ -76,12 +77,12 @@ def tile_nn_kernel(tc, state_grid, w_hidden_words, w_hidden_scales, w_out_words,
             for b in range(TOGETHER):
                 state[first_image + b] = raw[:, b]
 
-        def load_planes(planes, scales):
+        def load_planes(planes, scales, queues):
             passes = scales.shape[0]
-            for quadrant in range(4):
-                nc.sync.dma_start(
-                    out=planes[32 * quadrant : 32 * quadrant + 4 * passes, :].bitcast(I32),
-                    in_=scales[:, 4 * quadrant : 4 * quadrant + 4, :].bitcast(I32),
+            for quadrant, (queue, word) in enumerate(queues):
+                queue.dma_start(
+                    out=planes[32 * quadrant : 32 * quadrant + 4 * passes, :].bitcast(word),
+                    in_=scales[:, 4 * quadrant : 4 * quadrant + 4, :].bitcast(word),
                 )
 
         wh_bytes = w_hidden_words.rearrange("f p n t -> p f (n t)")
@@ -97,33 +98,36 @@ def tile_nn_kernel(tc, state_grid, w_hidden_words, w_hidden_scales, w_out_words,
 
         load_images(0)
         load_block(0)
-        load_planes(wh_planes_raw, w_hidden_scales)
+        load_planes(wh_planes_raw, w_hidden_scales, [(nc.sync, I32), (nc.scalar, F32)] * 2)
         load_block(1)
         load_block(2)
         load_block(3)
         load_images(TOGETHER)
-        load_planes(wo_planes, w_out_scales)
-        wo_words = keep.tile([P, HIDDEN_PASSES, CHANNELS], U32, align_bytes=64)
-        nc.sync.dma_start(
-            out=wo_words[:].bitcast(I32), in_=w_out_words.rearrange("g p n t -> p g (n t)").bitcast(I32)
-        )
-        square_raw = [
-            keep.tile([P, BLOCKS, QUARTER], BF16, name="square_raw%d" % b, align_bytes=64) for b in range(TOGETHER)
-        ]
-        for b in range(TOGETHER):
-            rows = state_rows[(TOGETHER + b) * IMAGE : (TOGETHER + b + 1) * IMAGE, :]
+        square_raw = {}
+
+        def load_squares(b):
+            square_raw[b] = keep.tile([P, BLOCKS, QUARTER], BF16, name="square_raw%d" % b, align_bytes=64)
+            rows = state_rows[b * IMAGE : (b + 1) * IMAGE, :]
             for quadrant in range(4):
                 nc.sync.dma_start(
                     out=square_raw[b][SQUARE * quadrant : SQUARE * (quadrant + 1)],
                     in_=rows[:, quadrant * QUARTER : (quadrant + 1) * QUARTER].rearrange("(k p) c -> p k c", p=SQUARE),
                 )
 
+        load_squares(2)
+        load_planes(wo_planes, w_out_scales, [(nc.sync, I32)] * 4)
+        wo_words = keep.tile([P, HIDDEN_PASSES, CHANNELS], U32, align_bytes=64)
+        nc.sync.dma_start(
+            out=wo_words[:].bitcast(I32), in_=w_out_words.rearrange("g p n t -> p g (n t)").bitcast(I32)
+        )
+        load_squares(3)
+
         ident_bf16 = keep.tile([P, P], BF16)
         make_identity(nc, ident_bf16[:])
 
         idle = sums.tile([P, BANK], F32, name="idle", tag="sums")
         for n in range(WARM_UP):
-            nc.tensor.matmul(out=idle[:], lhsT=nothing[:, :P], rhs=nothing[:], start=True, stop=True)
+            nc.tensor.matmul(out=idle[:, :P], lhsT=nothing[:], rhs=nothing[:], start=True, stop=True)
 
         padded = keep.tile([P, WINDOW_ROWS, PADDED], BF16)
         nc.vector.tensor_copy(out=padded[:, :, 1 : 1 + SIDE], in_=ident_bf16[:].rearrange("k (a c) -> k a c", c=SIDE))
@@ -243,7 +247,7 @@ def tile_nn_kernel(tc, state_grid, w_hidden_words, w_hidden_scales, w_out_words,
             squares[b] = work.tile([P, BLOCKS, 2, SQUARE], I32, name="by_word%d" % b, tag="by_word", align_bytes=64)
             nc.vector.tensor_copy(
                 out=squares[b][:],
-                in_=square_raw[b - TOGETHER][:].bitcast(I32).rearrange("p k (r v) -> p k v r", v=2),
+                in_=square_raw[b][:].bitcast(I32).rearrange("p k (r v) -> p k v r", v=2),
             )
 
         def turn_squares(b):
@@ -269,7 +273,13 @@ def tile_nn_kernel(tc, state_grid, w_hidden_words, w_hidden_scales, w_out_words,
                 in_=perception[b][:, filters].rearrange("p f q t -> p (f q t)"),
             )
 
-        def first_layer(b, g, u, on_scalar):
+        def relu_out(place, bank, on_scalar):
+            if on_scalar:
+                nc.scalar.activation(out=place, in_=bank, func=RELU)
+            else:
+                nc.vector.tensor_scalar_max(out=place, in0=bank, scalar1=0.0)
+
+        def first_layer(b, g, u, on_scalar, split=False):
             bank = banks.tile([P, PAIR, IMAGE], F32, tag="bank")
             for e in range(PAIR):
                 t = PAIR * u + e
@@ -286,22 +296,28 @@ def tile_nn_kernel(tc, state_grid, w_hidden_words, w_hidden_scales, w_out_words,
                     )
             place = hidden[b][:, g, :, PAIR * u : PAIR * (u + 1)]
             side_by_side = bank[:].rearrange("p e q -> p q e")
-            if on_scalar:
-                nc.scalar.activation(out=place, in_=side_by_side, func=RELU)
+            if split:
+                for half in range(HALVES):
+                    pixels = slice(half * P, (half + 1) * P)
+                    relu_out(place[:, pixels], side_by_side[:, pixels], half == 0)
             else:
-                nc.vector.tensor_scalar_max(out=place, in0=side_by_side, scalar1=0.0)
+                relu_out(place, side_by_side, on_scalar)
 
-        def quantise_hidden(b, g):
+        def quantise_hidden(b, g, pixels=slice(0, IMAGE)):
             nc.vector.quantize_mx(
-                out=hidden_words[b][:, g, :].bitcast(FP8X4),
-                scales=hidden_scales[b][:, g, :],
-                in_=hidden[b][:, g].rearrange("p q t -> p (q t)"),
+                out=hidden_words[b][:, g, pixels].bitcast(FP8X4),
+                scales=hidden_scales[b][:, g, pixels],
+                in_=hidden[b][:, g, pixels].rearrange("p q t -> p (q t)"),
             )
 
-        def second_layer(b, g):
-            for half in range(HALVES):
+        def second_layer(b, g, halves=range(HALVES)):
+            for half in halves:
                 if g == 0:
-                    out_sums[b, half] = sums.tile([P, CHANNELS], F32, name="sums%d_%d" % (b, half), tag="sums")
+                    out_sums[b, half] = (
+                        banks.tile([P, CHANNELS], F32, name="sums%d_%d" % (b, half), tag="bank")
+                        if b == IMAGES - 1
+                        else sums.tile([P, CHANNELS], F32, name="sums%d_%d" % (b, half), tag="sums")
+                    )
                 nc.tensor.matmul_mx(
                     out=out_sums[b, half][:],
                     lhsT=hidden_words[b][:, g, half * P : (half + 1) * P].bitcast(FP8X4),
@@ -344,19 +360,20 @@ def tile_nn_kernel(tc, state_grid, w_hidden_words, w_hidden_scales, w_out_words,
 
         slots = [(0, 0), (1, 0), (0, 1), (1, 1), (0, 2), (0, 3), (1, 2), (1, 3)]
         slots += [(b, g) for b in range(2, IMAGES) for g in range(HIDDEN_PASSES)]
-        tensor_extras = {(5,0): [(sobel_window, 2, 0, True)], (5,1): [(sobel_window, 2, 1, True)], (6,0): [(sobel_window, 2, 2, True), (second_layer, 0, 0)], (6,1): [(second_layer, 0, 1)], (7,0): [(second_layer, 0, 2)], (7,1): [(second_layer, 0, 3), (store, 0, 0, True, nc.sync), (store, 0, 1, False, nc.sync)], (9,0): [(second_layer, 1, 0), (sobel_window, 3, 2, True)], (9,1): [(second_layer, 1, 1)], (10,0): [(second_layer, 1, 2)], (10,1): [(second_layer, 1, 3), (store, 1, 0, True, nc.sync), (store, 1, 1, False, nc.sync)], (8,0): [(sobel_window, 3, 0, True)], (8,1): [(sobel_window, 3, 1, True)], (13,0): [(second_layer, 2, 0)], (13,1): [(second_layer, 2, 1)], (14,0): [(second_layer, 2, 2)], (14,1): [(second_layer, 2, 3), (store, 2, 0, True, nc.sync), (store, 2, 1, False, nc.sync)]}
+        tensor_extras = {(5,1): [(sobel_window, 2, 0, True), (sobel_window, 2, 1, False), (sobel_window, 2, 2, True)], (7,0): [(second_layer, 0, 0)], (7,1): [(second_layer, 0, 1)], (8,0): [(second_layer, 0, 2)], (8,1): [(second_layer, 0, 3), (store, 0, 0, True, nc.sync), (store, 0, 1, False, nc.sync), (sobel_window, 3, 0, True), (sobel_window, 3, 1, False), (sobel_window, 3, 2, True)], (10,0): [(second_layer, 1, 0)], (10,1): [(second_layer, 1, 1)], (11,0): [(second_layer, 1, 2)], (11,1): [(second_layer, 1, 3), (store, 1, 0, True, nc.sync), (store, 1, 1, False, nc.sync)], (13,0): [(second_layer, 2, 0)], (13,1): [(second_layer, 2, 1)], (14,0): [(second_layer, 2, 2)], (14,1): [(second_layer, 2, 3), (store, 2, 0, True, nc.sync), (store, 2, 1, False, nc.sync)]}
         vector_extras = {0: [(sort_hidden_units, 1)], 2: [(sort_hidden_units, 2)], 3: [(sort_hidden_units, 3)], 5: [(sort_words, 2)], 6: [(turn_squares, 2), (lay_state, 2), (quantise_perception, 2, STATE_ONLY), (quantise_perception, 2, BOTH_SOBELS)], 8: [(sort_words, 3)], 9: [(turn_squares, 3), (lay_state, 3)], 10: [(quantise_perception, 3, STATE_ONLY), (quantise_perception, 3, BOTH_SOBELS)]}
         for k, (b, g) in enumerate(slots):
             for u in range(PAIR):
-                first_layer(b, g, u, on_scalar=(u == 1 or k in (2, 3, 4)))
+                first_layer(b, g, u, on_scalar=(u == 1 or k in (0, 2, 3, 4)), split=(k == 15 and u == 1))
+                if u == 0 and k > 0:
+                    quantise_hidden(*slots[k - 1])
                 for call, *args in tensor_extras.get((k, u), ()):
                     call(*args)
             for call, *args in vector_extras.get(k, ()):
                 call(*args)
-            if k > 0:
-                quantise_hidden(*slots[k - 1])
-        quantise_hidden(3, HIDDEN_PASSES - 1)
-        for g in range(0, HIDDEN_PASSES):
-            second_layer(3, g)
+        for half in range(HALVES):
+            quantise_hidden(3, HIDDEN_PASSES - 1, slice(half * P, (half + 1) * P))
+        for half, g in ((0, 0), (0, 1), (0, 2), (1, 0), (1, 1), (0, 3), (1, 2), (1, 3)):
+            second_layer(3, g, (half,))
         store(3, 0, on_scalar=True, queue=nc.scalar)
         store(3, 1, on_scalar=False, queue=nc.sync)

@@ -57,16 +57,15 @@ def tile_nn_kernel(tc, state_grid, w_hidden_words, w_hidden_scales, w_out_words,
         wo_planes = keep.tile([P, CHANNELS], U8, align_bytes=64)
         nothing = keep.tile([P, P], BF16)
         nc.vector.memset(nothing[:], 0.0)
-        nc.scalar.activation(out=keep.tile([P, P], BF16, name="table")[:], in_=nothing[:], func=RELU)
         nc.vector.memset(wh_planes_raw[:].bitcast(I32), 0)
         nc.vector.memset(wo_planes[:].bitcast(I32), 0)
 
         state = {}
 
-        def load_images(first_image):
-            raw = keep.tile([P, TOGETHER, WINDOWS, CHANNELS], BF16, name="state%d" % first_image)
-            rows = state_rows[first_image * IMAGE : (first_image + TOGETHER) * IMAGE, :].rearrange(
-                "(b q) c -> q b c", b=TOGETHER
+        def load_images(first_image, together):
+            raw = keep.tile([P, together, WINDOWS, CHANNELS], BF16, name="state%d" % first_image)
+            rows = state_rows[first_image * IMAGE : (first_image + together) * IMAGE, :].rearrange(
+                "(b q) c -> q b c", b=together
             )
             for w in range(WINDOWS):
                 first = (FIRST_ROW[first_image] - 1 + INNER_ROWS * w) % SIDE * SIDE
@@ -74,16 +73,14 @@ def tile_nn_kernel(tc, state_grid, w_hidden_words, w_hidden_scales, w_out_words,
                 nc.sync.dma_start(out=raw[:inside, :, w, :], in_=rows[first : first + inside])
                 if inside < P:
                     nc.sync.dma_start(out=raw[inside:, :, w, :], in_=rows[: P - inside])
-            for b in range(TOGETHER):
+            for b in range(together):
                 state[first_image + b] = raw[:, b]
 
-        def load_planes(planes, scales, queues):
-            passes = scales.shape[0]
-            for quadrant, (queue, word) in enumerate(queues):
-                queue.dma_start(
-                    out=planes[32 * quadrant : 32 * quadrant + 4 * passes, :].bitcast(word),
-                    in_=scales[:, 4 * quadrant : 4 * quadrant + 4, :].bitcast(word),
-                )
+        def load_planes(planes, scales, quadrant, queue, word):
+            queue.dma_start(
+                out=planes[32 * quadrant : 32 * quadrant + 4 * scales.shape[0], :].bitcast(word),
+                in_=scales[:, 4 * quadrant : 4 * quadrant + 4, :].bitcast(word),
+            )
 
         wh_bytes = w_hidden_words.rearrange("f p n t -> p f (n t)")
         wh_raw = []
@@ -96,13 +93,6 @@ def tile_nn_kernel(tc, state_grid, w_hidden_words, w_hidden_scales, w_out_words,
             )
             wh_raw.append(block)
 
-        load_images(0)
-        load_block(0)
-        load_planes(wh_planes_raw, w_hidden_scales, [(nc.sync, I32), (nc.scalar, F32)] * 2)
-        load_block(1)
-        load_block(2)
-        load_block(3)
-        load_images(TOGETHER)
         square_raw = {}
 
         def load_squares(b):
@@ -114,12 +104,21 @@ def tile_nn_kernel(tc, state_grid, w_hidden_words, w_hidden_scales, w_out_words,
                     in_=rows[:, quadrant * QUARTER : (quadrant + 1) * QUARTER].rearrange("(k p) c -> p k c", p=SQUARE),
                 )
 
-        load_squares(2)
-        load_planes(wo_planes, w_out_scales, [(nc.sync, I32)] * 4)
         wo_words = keep.tile([P, HIDDEN_PASSES, CHANNELS], U32, align_bytes=64)
+        load_images(0, 2)
+        load_block(0)
+        for quadrant in range(4):
+            load_planes(wh_planes_raw, w_hidden_scales, quadrant, nc.sync, I32)
+        load_block(1)
+        load_block(2)
+        load_block(3)
+        load_images(2, 1)
+        for quadrant in range(4):
+            load_planes(wo_planes, w_out_scales, quadrant, nc.sync, I32)
         nc.sync.dma_start(
             out=wo_words[:].bitcast(I32), in_=w_out_words.rearrange("g p n t -> p g (n t)").bitcast(I32)
         )
+        load_images(3, 1)
         load_squares(3)
 
         ident_bf16 = keep.tile([P, P], BF16)
@@ -303,6 +302,23 @@ def tile_nn_kernel(tc, state_grid, w_hidden_words, w_hidden_scales, w_out_words,
             else:
                 relu_out(place, side_by_side, on_scalar)
 
+        def first_layer_tile(b, g, half, on_scalar):
+            pixels = slice(half * P, (half + 1) * P)
+            bank = banks.tile([P, PACK, P], F32, tag="bank")
+            for t in range(PACK):
+                first = (g * PACK + t) * P
+                for f in PASS_ORDER:
+                    nc.tensor.matmul_mx(
+                        out=bank[:, t, :],
+                        lhsT=wh_words[g][:, f, t, :].bitcast(FP8X4),
+                        lhsT_scale=wh_planes[4 * f : P, first : first + P],
+                        rhs=perception_words[b][:, f, pixels].bitcast(FP8X4),
+                        rhs_scale=perception_scales[b][:, f, pixels],
+                        start=(f == PASS_ORDER[0]),
+                        stop=(f == PASS_ORDER[-1]),
+                    )
+            relu_out(hidden[b][:, g, pixels, :], bank[:].rearrange("p t q -> p q t"), on_scalar)
+
         def quantise_hidden(b, g, pixels=slice(0, IMAGE)):
             nc.vector.quantize_mx(
                 out=hidden_words[b][:, g, pixels].bitcast(FP8X4),
@@ -310,32 +326,32 @@ def tile_nn_kernel(tc, state_grid, w_hidden_words, w_hidden_scales, w_out_words,
                 in_=hidden[b][:, g, pixels].rearrange("p q t -> p (q t)"),
             )
 
-        def second_layer(b, g, halves=range(HALVES)):
+        def second_layer(b, g, halves=range(HALVES), columns=slice(0, CHANNELS)):
             for half in halves:
+                key = (b, half, columns.start)
                 if g == 0:
-                    out_sums[b, half] = (
-                        banks.tile([P, CHANNELS], F32, name="sums%d_%d" % (b, half), tag="bank")
-                        if b == IMAGES - 1
-                        else sums.tile([P, CHANNELS], F32, name="sums%d_%d" % (b, half), tag="sums")
-                    )
+                    pool, tag = (banks, "bank") if b == IMAGES - 1 else (sums, "sums")
+                    out_sums[key] = pool.tile([P, columns.stop - columns.start], F32, name="sums%d_%d_%d" % key, tag=tag)
                 nc.tensor.matmul_mx(
-                    out=out_sums[b, half][:],
+                    out=out_sums[key][:],
                     lhsT=hidden_words[b][:, g, half * P : (half + 1) * P].bitcast(FP8X4),
                     lhsT_scale=hidden_scales[b][:, g, half * P : (half + 1) * P],
-                    rhs=wo_words[:, g, :].bitcast(FP8X4),
-                    rhs_scale=wo_planes[4 * g : P, :],
+                    rhs=wo_words[:, g, columns].bitcast(FP8X4),
+                    rhs_scale=wo_planes[4 * g : P, columns],
                     start=(g == 0),
                     stop=(g == HIDDEN_PASSES - 1),
                 )
 
-        def store(b, half, on_scalar, queue):
-            result = work.tile([P, CHANNELS], F32, name="result%d_%d" % (b, half), tag="result", bufs=4)
-            copy_out(result[:], out_sums[b, half][:], on_scalar)
+        def store(b, half, on_scalar, queue, columns=slice(0, CHANNELS)):
+            key = (b, half, columns.start)
+            result = work.tile([P, columns.stop - columns.start], F32, name="result%d_%d_%d" % key, tag="result", bufs=4)
+            copy_out(result[:], out_sums[key][:], on_scalar)
             first = half * P + FIRST_ROW[b] * SIDE
             inside = min(P, IMAGE - first)
-            queue.dma_start(out=out_rows[b * IMAGE + first : b * IMAGE + first + inside, :], in_=result[:inside, :])
+            rows = out_rows[b * IMAGE : (b + 1) * IMAGE, columns]
+            queue.dma_start(out=rows[first : first + inside], in_=result[:inside, :])
             if inside < P:
-                queue.dma_start(out=out_rows[b * IMAGE : b * IMAGE + P - inside, :], in_=result[inside:, :])
+                queue.dma_start(out=rows[: P - inside], in_=result[inside:, :])
 
         STATE_ONLY = slice(STATE, FILTERS)
         BOTH_SOBELS = slice(0, SOBELS)
@@ -358,22 +374,32 @@ def tile_nn_kernel(tc, state_grid, w_hidden_words, w_hidden_scales, w_out_words,
         quantise_perception(1, BOTH_SOBELS)
         quantise_perception(1, STATE_ONLY)
 
-        slots = [(0, 0), (1, 0), (0, 1), (1, 1), (0, 2), (0, 3), (1, 2), (1, 3)]
+        slots = [(0, 0), (1, 0), (0, 1), (1, 1), (0, 2), (1, 2), (0, 3), (1, 3)]
         slots += [(b, g) for b in range(2, IMAGES) for g in range(HIDDEN_PASSES)]
-        tensor_extras = {(5,1): [(sobel_window, 2, 0, True), (sobel_window, 2, 1, False), (sobel_window, 2, 2, True)], (7,0): [(second_layer, 0, 0)], (7,1): [(second_layer, 0, 1)], (8,0): [(second_layer, 0, 2)], (8,1): [(second_layer, 0, 3), (store, 0, 0, True, nc.sync), (store, 0, 1, False, nc.sync), (sobel_window, 3, 0, True), (sobel_window, 3, 1, False), (sobel_window, 3, 2, True)], (10,0): [(second_layer, 1, 0)], (10,1): [(second_layer, 1, 1)], (11,0): [(second_layer, 1, 2)], (11,1): [(second_layer, 1, 3), (store, 1, 0, True, nc.sync), (store, 1, 1, False, nc.sync)], (13,0): [(second_layer, 2, 0)], (13,1): [(second_layer, 2, 1)], (14,0): [(second_layer, 2, 2)], (14,1): [(second_layer, 2, 3), (store, 2, 0, True, nc.sync), (store, 2, 1, False, nc.sync)]}
-        vector_extras = {0: [(sort_hidden_units, 1)], 2: [(sort_hidden_units, 2)], 3: [(sort_hidden_units, 3)], 5: [(sort_words, 2)], 6: [(turn_squares, 2), (lay_state, 2), (quantise_perception, 2, STATE_ONLY), (quantise_perception, 2, BOTH_SOBELS)], 8: [(sort_words, 3)], 9: [(turn_squares, 3), (lay_state, 3)], 10: [(quantise_perception, 3, STATE_ONLY), (quantise_perception, 3, BOTH_SOBELS)]}
+        tensor_extras = {(5,0): [(state_window, 2, 0), (state_window, 2, 1), (state_window, 2, 2), (state_out, 2, True)], (5,1): [(sobel_window, 2, 0, True), (sobel_window, 2, 1, False), (sobel_window, 2, 2, True)], (7,1): [(second_layer, 0, 0)], (8,0): [(second_layer, 0, 1)], (8,1): [(second_layer, 0, 2), (sobel_window, 3, 0, True), (sobel_window, 3, 1, False), (sobel_window, 3, 2, True)], (9,0): [(second_layer, 0, 3), (store, 0, 0, True, nc.sync), (store, 0, 1, False, nc.sync)], (10,0): [(second_layer, 1, 0)], (10,1): [(second_layer, 1, 1)], (11,0): [(second_layer, 1, 2)], (11,1): [(second_layer, 1, 3), (store, 1, 0, True, nc.sync), (store, 1, 1, False, nc.sync)], (13,0): [(second_layer, 2, 0)], (13,1): [(second_layer, 2, 1)], (14,0): [(second_layer, 2, 2)], (14,1): [(second_layer, 2, 3), (store, 2, 0, True, nc.sync), (store, 2, 1, False, nc.sync)]}
+        vector_extras = {0: [(sort_hidden_units, 1)], 2: [(sort_hidden_units, 2)], 4: [(sort_hidden_units, 3)], 6: [(quantise_perception, 2, STATE_ONLY), (quantise_perception, 2, BOTH_SOBELS)], 8: [(sort_words, 3)], 9: [(turn_squares, 3), (lay_state, 3)], 10: [(quantise_perception, 3, STATE_ONLY), (quantise_perception, 3, BOTH_SOBELS)]}
         for k, (b, g) in enumerate(slots):
             for u in range(PAIR):
-                first_layer(b, g, u, on_scalar=(u == 1 or k in (0, 2, 3, 4)), split=(k == 15 and u == 1))
+                if k == 15:
+                    first_layer_tile(b, g, u, on_scalar=True)
+                else:
+                    first_layer(b, g, u, on_scalar=(u == 1 or k in (0, 2, 4)))
                 if u == 0 and k > 0:
                     quantise_hidden(*slots[k - 1])
+                if u == 0 and k == 15:
+                    quantise_hidden(b, g, slice(0, P))
                 for call, *args in tensor_extras.get((k, u), ()):
                     call(*args)
             for call, *args in vector_extras.get(k, ()):
                 call(*args)
-        for half in range(HALVES):
-            quantise_hidden(3, HIDDEN_PASSES - 1, slice(half * P, (half + 1) * P))
-        for half, g in ((0, 0), (0, 1), (0, 2), (1, 0), (1, 1), (0, 3), (1, 2), (1, 3)):
-            second_layer(3, g, (half,))
+        quantise_hidden(3, 3, slice(P, IMAGE))
+        left, right = slice(0, CHANNELS // 2), slice(CHANNELS // 2, CHANNELS)
+        for g in range(HIDDEN_PASSES):
+            second_layer(3, g, (0,))
         store(3, 0, on_scalar=True, queue=nc.scalar)
-        store(3, 1, on_scalar=False, queue=nc.sync)
+        for g in range(HIDDEN_PASSES):
+            second_layer(3, g, (1,), left)
+        store(3, 1, on_scalar=False, queue=nc.sync, columns=left)
+        for g in range(HIDDEN_PASSES):
+            second_layer(3, g, (1,), right)
+        store(3, 1, on_scalar=False, queue=nc.sync, columns=right)

@@ -23,8 +23,6 @@ HALVES = IMAGE // P
 WINDOW_ROWS = P // SIDE
 INNER_ROWS = WINDOW_ROWS - 2
 WINDOWS = 3
-TOGETHER = 2
-FIRST_ROW = (1, 1, 0, 0)
 FILTERS = 3
 SOBELS = 2
 STATE = 2
@@ -53,6 +51,9 @@ def tile_nn_kernel(tc, state_grid, w_hidden_words, w_hidden_scales, w_out_words,
         banks = stack.enter_context(tc.psum_pool(name="banks", bufs=6))
         sums = stack.enter_context(tc.psum_pool(name="sums", bufs=2))
 
+        ident_bf16 = keep.tile([P, P], BF16)
+        make_identity(nc, ident_bf16[:])
+
         wh_planes_raw = keep.tile([P, HIDDEN], U8, align_bytes=64)
         wo_planes = keep.tile([P, CHANNELS], U8, align_bytes=64)
         nothing = keep.tile([P, P], BF16)
@@ -63,18 +64,19 @@ def tile_nn_kernel(tc, state_grid, w_hidden_words, w_hidden_scales, w_out_words,
         state = {}
 
         def load_images(first_image, together):
-            raw = keep.tile([P, together, WINDOWS, CHANNELS], BF16, name="state%d" % first_image)
+            raw = [
+                keep.tile([P, together, CHANNELS], BF16, name="state%d_%d" % (first_image, w)) for w in range(WINDOWS)
+            ]
             rows = state_rows[first_image * IMAGE : (first_image + together) * IMAGE, :].rearrange(
                 "(b q) c -> q b c", b=together
             )
-            for w in range(WINDOWS):
-                first = (FIRST_ROW[first_image] - 1 + INNER_ROWS * w) % SIDE * SIDE
-                inside = min(P, IMAGE - first)
-                nc.sync.dma_start(out=raw[:inside, :, w, :], in_=rows[first : first + inside])
-                if inside < P:
-                    nc.sync.dma_start(out=raw[inside:, :, w, :], in_=rows[: P - inside])
+            for w in range(WINDOWS - 1):
+                first = INNER_ROWS * w * SIDE
+                nc.sync.dma_start(out=raw[w][:], in_=rows[first : first + P])
+            nc.sync.dma_start(out=raw[-1][0::2], in_=rows[IMAGE - P // 2 :])
+            nc.sync.dma_start(out=raw[-1][1::2], in_=rows[: P // 2])
             for b in range(together):
-                state[first_image + b] = raw[:, b]
+                state[first_image + b] = [window[:, b] for window in raw]
 
         def load_planes(planes, scales, quadrant, queue, word):
             queue.dma_start(
@@ -121,41 +123,41 @@ def tile_nn_kernel(tc, state_grid, w_hidden_words, w_hidden_scales, w_out_words,
         load_images(3, 1)
         load_squares(3)
 
-        ident_bf16 = keep.tile([P, P], BF16)
-        make_identity(nc, ident_bf16[:])
-
         idle = sums.tile([P, BANK], F32, name="idle", tag="sums")
         for n in range(WARM_UP):
             nc.tensor.matmul(out=idle[:, :P], lhsT=nothing[:], rhs=nothing[:], start=True, stop=True)
 
-        padded = keep.tile([P, WINDOW_ROWS, PADDED], BF16)
-        nc.vector.tensor_copy(out=padded[:, :, 1 : 1 + SIDE], in_=ident_bf16[:].rearrange("k (a c) -> k a c", c=SIDE))
-        nc.vector.tensor_copy(out=padded[:, :, 0:1], in_=padded[:, :, SIDE : SIDE + 1])
-        nc.vector.tensor_copy(out=padded[:, :, SIDE + 1 :], in_=padded[:, :, 1:2])
+        def build_taps(name, identity, inner_rows):
+            rows = inner_rows + 2
+            padded = keep.tile([P, WINDOW_ROWS, PADDED], BF16, name="padded_" + name)
+            nc.vector.tensor_copy(out=padded[:, :, 1 : 1 + SIDE].rearrange("k (h a) c -> k h a c", h=2), in_=identity)
+            nc.vector.tensor_copy(out=padded[:, :, 0:1], in_=padded[:, :, SIDE : SIDE + 1])
+            nc.vector.tensor_copy(out=padded[:, :, SIDE + 1 :], in_=padded[:, :, 1:2])
+            taps = keep.tile([P, FILTERS, inner_rows, SIDE], BF16, name="taps_" + name)
+            diff_x = keep.tile([P, rows, SIDE], BF16, name="diff_x_" + name)
+            part_x = keep.tile([P, inner_rows, SIDE], BF16, name="part_x_" + name)
+            part_y = keep.tile([P, rows, SIDE], BF16, name="part_y_" + name)
+            sum_y = keep.tile([P, rows, SIDE], BF16, name="sum_y_" + name)
+            left, centre, right = (padded[:, :rows, j : j + SIDE] for j in range(3))
+            nc.vector.tensor_sub(out=diff_x[:], in0=right, in1=left)
+            nc.vector.tensor_copy(out=taps[:, STATE], in_=centre[:, 1 : 1 + inner_rows, :])
+            nc.vector.scalar_tensor_tensor(out=part_y[:], in0=centre, scalar=2.0, in1=left, op0=ALU.mult, op1=ALU.add)
+            nc.vector.scalar_tensor_tensor(
+                out=part_x[:],
+                in0=diff_x[:, 1 : 1 + inner_rows, :],
+                scalar=2.0,
+                in1=diff_x[:, :inner_rows, :],
+                op0=ALU.mult,
+                op1=ALU.add,
+            )
+            nc.vector.tensor_add(out=sum_y[:], in0=part_y[:], in1=right)
+            nc.vector.tensor_add(out=taps[:, 0], in0=part_x[:], in1=diff_x[:, 2:, :])
+            nc.vector.tensor_sub(out=taps[:, 1], in0=sum_y[:, 2:, :], in1=sum_y[:, :inner_rows, :])
+            return taps[:].rearrange("k f o j -> k f (o j)")
 
-        taps = keep.tile([P, SOBELS, INNER_ROWS * SIDE], BF16)
-        diff_x = keep.tile([P, WINDOW_ROWS, SIDE], BF16)
-        part_x = keep.tile([P, INNER_ROWS, SIDE], BF16)
-        part_y = keep.tile([P, WINDOW_ROWS, SIDE], BF16)
-        sum_y = keep.tile([P, WINDOW_ROWS, SIDE], BF16)
-        nc.vector.tensor_sub(out=diff_x[:], in0=padded[:, :, 2:], in1=padded[:, :, :SIDE])
-        nc.vector.scalar_tensor_tensor(
-            out=part_y[:], in0=padded[:, :, 1 : 1 + SIDE], scalar=2.0, in1=padded[:, :, :SIDE], op0=ALU.mult, op1=ALU.add
-        )
-        nc.vector.scalar_tensor_tensor(
-            out=part_x[:],
-            in0=diff_x[:, 1 : 1 + INNER_ROWS, :],
-            scalar=2.0,
-            in1=diff_x[:, :INNER_ROWS, :],
-            op0=ALU.mult,
-            op1=ALU.add,
-        )
-        nc.vector.tensor_add(out=sum_y[:], in0=part_y[:], in1=padded[:, :, 2:])
-        nc.vector.tensor_add(
-            out=taps[:, 0, :].rearrange("k (o j) -> k o j", j=SIDE), in0=part_x[:], in1=diff_x[:, 2:, :]
-        )
-        nc.vector.tensor_sub(
-            out=taps[:, 1, :].rearrange("k (o j) -> k o j", j=SIDE), in0=sum_y[:, 2:, :], in1=sum_y[:, :INNER_ROWS, :]
+        taps = [build_taps("plain", ident_bf16[:].rearrange("k (h a c) -> k h a c", h=2, c=SIDE), INNER_ROWS)] * 2
+        taps.append(
+            build_taps("woven", ident_bf16[:].rearrange("k (a c h) -> k h a c", h=2, c=SIDE), SIDE - 2 * INNER_ROWS)
         )
 
         wh_planes = keep.tile([P, HIDDEN], U8, align_bytes=64)
@@ -206,8 +208,15 @@ def tile_nn_kernel(tc, state_grid, w_hidden_words, w_hidden_scales, w_out_words,
             first = INNER_ROWS * w * SIDE
             return first, min(INNER_ROWS * SIDE, IMAGE - first)
 
+        def round_the_grid(first, width):
+            inside = min(width, IMAGE - SIDE - first)
+            parts = [(slice(first + SIDE, first + SIDE + inside), slice(0, inside))]
+            if inside < width:
+                parts.append((slice(0, width - inside), slice(inside, width)))
+            return parts
+
         def channels_of(b, w, t):
-            return state[b][:, w, :].rearrange("q (p t) -> q t p", t=PACK)[:, t, :]
+            return state[b][w].rearrange("q (p t) -> q t p", t=PACK)[:, t, :]
 
         def copy_out(place, bank, on_scalar):
             if on_scalar:
@@ -223,24 +232,26 @@ def tile_nn_kernel(tc, state_grid, w_hidden_words, w_hidden_scales, w_out_words,
                 nc.tensor.matmul(
                     out=state_banks[b][:, t, first : first + width],
                     lhsT=channels_of(b, w, t),
-                    rhs=ident_bf16[:, SIDE : SIDE + width],
+                    rhs=taps[w][:, STATE],
                     start=True,
                     stop=True,
                 )
 
         def state_out(b, on_scalar):
-            copy_out(perception[b][:, STATE], state_banks[b][:].rearrange("p t q -> p q t"), on_scalar)
+            for place, part in round_the_grid(0, IMAGE):
+                copy_out(perception[b][:, STATE, place], state_banks[b][:, :, part].rearrange("p t q -> p q t"), on_scalar)
 
         def sobel_window(b, w, on_scalar):
             first, width = inner(w)
             bank = banks.tile([P, PACK, SOBELS, width], BF16, tag="bank")
             for t in range(PACK):
                 nc.tensor.matmul(
-                    out=bank[:, t], lhsT=channels_of(b, w, t), rhs=taps[:, :, :width], start=True, stop=True
+                    out=bank[:, t], lhsT=channels_of(b, w, t), rhs=taps[w][:, :SOBELS], start=True, stop=True
                 )
-            copy_out(
-                perception[b][:, :SOBELS, first : first + width, :], bank[:].rearrange("p t f q -> p f q t"), on_scalar
-            )
+            for place, part in round_the_grid(first, width):
+                copy_out(
+                    perception[b][:, :SOBELS, place, :], bank[:, :, :, part].rearrange("p t f q -> p f q t"), on_scalar
+                )
 
         def sort_words(b):
             squares[b] = work.tile([P, BLOCKS, 2, SQUARE], I32, name="by_word%d" % b, tag="by_word", align_bytes=64)
@@ -346,12 +357,8 @@ def tile_nn_kernel(tc, state_grid, w_hidden_words, w_hidden_scales, w_out_words,
             key = (b, half, columns.start)
             result = work.tile([P, columns.stop - columns.start], F32, name="result%d_%d_%d" % key, tag="result", bufs=4)
             copy_out(result[:], out_sums[key][:], on_scalar)
-            first = half * P + FIRST_ROW[b] * SIDE
-            inside = min(P, IMAGE - first)
-            rows = out_rows[b * IMAGE : (b + 1) * IMAGE, columns]
-            queue.dma_start(out=rows[first : first + inside], in_=result[:inside, :])
-            if inside < P:
-                queue.dma_start(out=rows[: P - inside], in_=result[inside:, :])
+            first = b * IMAGE + half * P
+            queue.dma_start(out=out_rows[first : first + P, columns], in_=result[:])
 
         STATE_ONLY = slice(STATE, FILTERS)
         BOTH_SOBELS = slice(0, SOBELS)

@@ -78,11 +78,12 @@ def tile_nn_kernel(tc, state_grid, w_hidden_words, w_hidden_scales, w_out_words,
             for b in range(together):
                 state[first_image + b] = [window[:, b] for window in raw]
 
-        def load_planes(planes, scales, quadrant, queue, word):
-            queue.dma_start(
-                out=planes[32 * quadrant : 32 * quadrant + 4 * scales.shape[0], :].bitcast(word),
-                in_=scales[:, 4 * quadrant : 4 * quadrant + 4, :].bitcast(word),
-            )
+        def load_planes(planes, scales, columns):
+            for quadrant in range(4):
+                nc.sync.dma_start(
+                    out=planes[32 * quadrant : 32 * quadrant + 4 * scales.shape[0], columns].bitcast(I32),
+                    in_=scales[:, 4 * quadrant : 4 * quadrant + 4, columns].bitcast(I32),
+                )
 
         wh_bytes = w_hidden_words.rearrange("f p n t -> p f (n t)")
         wh_raw = []
@@ -109,14 +110,13 @@ def tile_nn_kernel(tc, state_grid, w_hidden_words, w_hidden_scales, w_out_words,
         wo_words = keep.tile([P, HIDDEN_PASSES, CHANNELS], U32, align_bytes=64)
         load_images(0, 2)
         load_block(0)
-        for quadrant in range(4):
-            load_planes(wh_planes_raw, w_hidden_scales, quadrant, nc.sync, I32)
+        load_planes(wh_planes_raw, w_hidden_scales, slice(0, BANK))
         load_block(1)
+        load_planes(wh_planes_raw, w_hidden_scales, slice(BANK, HIDDEN))
         load_block(2)
         load_block(3)
         load_images(2, 1)
-        for quadrant in range(4):
-            load_planes(wo_planes, w_out_scales, quadrant, nc.sync, I32)
+        load_planes(wo_planes, w_out_scales, slice(0, CHANNELS))
         nc.sync.dma_start(
             out=wo_words[:].bitcast(I32), in_=w_out_words.rearrange("g p n t -> p g (n t)").bitcast(I32)
         )

@@ -90,10 +90,11 @@ def tile_nn_kernel(tc, state_grid, w_hidden_words, w_hidden_scales, w_out_words,
 
         def load_block(g):
             block = keep.tile([P, FILTERS, BANK], U32, name="wh_raw%d" % g, align_bytes=64)
-            nc.sync.dma_start(
-                out=block[:].bitcast(I32),
-                in_=wh_bytes[:, :, g * BANK * PACK : (g + 1) * BANK * PACK].bitcast(I32),
-            )
+            for filters in (slice(STATE, FILTERS), slice(0, SOBELS)) if g == 0 else (slice(0, FILTERS),):
+                nc.sync.dma_start(
+                    out=block[:, filters].bitcast(I32),
+                    in_=wh_bytes[:, filters, g * BANK * PACK : (g + 1) * BANK * PACK].bitcast(I32),
+                )
             wh_raw.append(block)
 
         square_raw = {}
@@ -123,9 +124,12 @@ def tile_nn_kernel(tc, state_grid, w_hidden_words, w_hidden_scales, w_out_words,
         load_images(3, 1)
         load_squares(3)
 
-        idle = sums.tile([P, BANK], F32, name="idle", tag="sums")
-        for n in range(WARM_UP):
-            nc.tensor.matmul(out=idle[:, :P], lhsT=nothing[:], rhs=nothing[:], start=True, stop=True)
+        def keep_busy(passes):
+            idle = sums.tile([P, P], F32, name="idle%d" % passes, tag="sums")
+            for n in range(passes):
+                nc.tensor.matmul(out=idle[:], lhsT=nothing[:], rhs=nothing[:], start=True, stop=True)
+
+        keep_busy(WARM_UP)
 
         def build_taps(name, identity, inner_rows):
             rows = inner_rows + 2
@@ -163,6 +167,7 @@ def tile_nn_kernel(tc, state_grid, w_hidden_words, w_hidden_scales, w_out_words,
         wh_planes = keep.tile([P, HIDDEN], U8, align_bytes=64)
         wh_words = {}
         state_banks = {}
+        sobel_banks = {}
         squares = {}
         out_sums = {}
         perception = [
@@ -200,9 +205,9 @@ def tile_nn_kernel(tc, state_grid, w_hidden_words, w_hidden_scales, w_out_words,
             )
 
         def sort_hidden_units(g):
-            sort_planes(g)
             for f in PASS_ORDER:
                 sort_block(g, f)
+            sort_planes(g)
 
         def inner(w):
             first = INNER_ROWS * w * SIDE
@@ -241,16 +246,20 @@ def tile_nn_kernel(tc, state_grid, w_hidden_words, w_hidden_scales, w_out_words,
             for place, part in round_the_grid(0, IMAGE):
                 copy_out(perception[b][:, STATE, place], state_banks[b][:, :, part].rearrange("p t q -> p q t"), on_scalar)
 
-        def sobel_window(b, w, on_scalar):
+        def sobel_window(b, w):
             first, width = inner(w)
-            bank = banks.tile([P, PACK, SOBELS, width], BF16, tag="bank")
+            bank = banks.tile([P, PACK, SOBELS, width], BF16, name="sobel_bank%d_%d" % (b, w), tag="bank")
+            sobel_banks[b, w] = bank
             for t in range(PACK):
                 nc.tensor.matmul(
                     out=bank[:, t], lhsT=channels_of(b, w, t), rhs=taps[w][:, :SOBELS], start=True, stop=True
                 )
+
+        def sobel_out(b, w, on_scalar):
+            first, width = inner(w)
             for place, part in round_the_grid(first, width):
                 copy_out(
-                    perception[b][:, :SOBELS, place, :], bank[:, :, :, part].rearrange("p t f q -> p f q t"), on_scalar
+                    perception[b][:, :SOBELS, place, :], sobel_banks[b, w][:, :, :, part].rearrange("p t f q -> p f q t"), on_scalar
                 )
 
         def sort_words(b):
@@ -355,7 +364,7 @@ def tile_nn_kernel(tc, state_grid, w_hidden_words, w_hidden_scales, w_out_words,
 
         def store(b, half, on_scalar, queue, columns=slice(0, CHANNELS)):
             key = (b, half, columns.start)
-            result = work.tile([P, columns.stop - columns.start], F32, name="result%d_%d_%d" % key, tag="result", bufs=4)
+            result = work.tile([P, columns.stop - columns.start], F32, name="result%d_%d_%d" % key, tag="result", bufs=2 * IMAGES + 2)
             copy_out(result[:], out_sums[key][:], on_scalar)
             first = b * IMAGE + half * P
             queue.dma_start(out=out_rows[first : first + P, columns], in_=result[:])
@@ -364,26 +373,31 @@ def tile_nn_kernel(tc, state_grid, w_hidden_words, w_hidden_scales, w_out_words,
         BOTH_SOBELS = slice(0, SOBELS)
         for w in range(WINDOWS):
             state_window(0, w)
-            if w == WINDOWS - 1:
-                state_out(0, on_scalar=True)
-            sobel_window(0, w, on_scalar=(w == 0))
+            sobel_window(0, w)
+        sobel_out(0, 0, on_scalar=True)
+        sobel_out(0, 1, on_scalar=False)
+        state_out(0, on_scalar=True)
+        sobel_out(0, 2, on_scalar=False)
+        sort_block(0, 2)
         quantise_perception(0, BOTH_SOBELS)
         quantise_perception(0, STATE_ONLY)
         for w in range(WINDOWS):
             state_window(1, w)
-            if w == WINDOWS - 1:
-                state_out(1, on_scalar=True)
-            sobel_window(1, w, on_scalar=True)
-        sort_block(0, 2)
-        sort_planes(0)
+            sobel_window(1, w)
+        keep_busy(8)
+        sobel_out(1, 0, on_scalar=True)
+        sobel_out(1, 1, on_scalar=True)
+        state_out(1, on_scalar=True)
         sort_block(0, 0)
+        sort_planes(0)
         sort_block(0, 1)
+        sobel_out(1, 2, on_scalar=False)
         quantise_perception(1, BOTH_SOBELS)
         quantise_perception(1, STATE_ONLY)
 
         slots = [(0, 0), (1, 0), (0, 1), (1, 1), (0, 2), (1, 2), (0, 3), (1, 3)]
         slots += [(b, g) for b in range(2, IMAGES) for g in range(HIDDEN_PASSES)]
-        tensor_extras = {(5,0): [(state_window, 2, 0), (state_window, 2, 1), (state_window, 2, 2), (state_out, 2, True)], (5,1): [(sobel_window, 2, 0, True), (sobel_window, 2, 1, False), (sobel_window, 2, 2, True)], (7,1): [(second_layer, 0, 0)], (8,0): [(second_layer, 0, 1)], (8,1): [(second_layer, 0, 2), (sobel_window, 3, 0, True), (sobel_window, 3, 1, False), (sobel_window, 3, 2, True)], (9,0): [(second_layer, 0, 3), (store, 0, 0, True, nc.sync), (store, 0, 1, False, nc.sync)], (10,0): [(second_layer, 1, 0)], (10,1): [(second_layer, 1, 1)], (11,0): [(second_layer, 1, 2)], (11,1): [(second_layer, 1, 3), (store, 1, 0, True, nc.sync), (store, 1, 1, False, nc.sync)], (13,0): [(second_layer, 2, 0)], (13,1): [(second_layer, 2, 1)], (14,0): [(second_layer, 2, 2)], (14,1): [(second_layer, 2, 3), (store, 2, 0, True, nc.sync), (store, 2, 1, False, nc.sync)]}
+        tensor_extras = {(5,0): [(state_window, 2, 0), (state_window, 2, 1), (state_window, 2, 2), (state_out, 2, True)], (5,1): [(sobel_window, 2, 0), (sobel_out, 2, 0, True), (sobel_window, 2, 1), (sobel_out, 2, 1, False), (sobel_window, 2, 2), (sobel_out, 2, 2, True)], (7,1): [(second_layer, 0, 0)], (8,0): [(second_layer, 0, 1)], (8,1): [(second_layer, 0, 2), (sobel_window, 3, 0), (sobel_out, 3, 0, True), (sobel_window, 3, 1), (sobel_out, 3, 1, False), (sobel_window, 3, 2), (sobel_out, 3, 2, True)], (9,0): [(second_layer, 0, 3), (store, 0, 0, True, nc.sync), (store, 0, 1, False, nc.sync)], (10,0): [(second_layer, 1, 0)], (10,1): [(second_layer, 1, 1)], (11,0): [(second_layer, 1, 2)], (11,1): [(second_layer, 1, 3), (store, 1, 0, True, nc.sync), (store, 1, 1, False, nc.sync)], (13,0): [(second_layer, 2, 0)], (13,1): [(second_layer, 2, 1)], (14,0): [(second_layer, 2, 2)], (14,1): [(second_layer, 2, 3), (store, 2, 0, True, nc.sync), (store, 2, 1, False, nc.sync)]}
         vector_extras = {0: [(sort_hidden_units, 1)], 2: [(sort_hidden_units, 2)], 4: [(sort_hidden_units, 3)], 6: [(quantise_perception, 2, STATE_ONLY), (quantise_perception, 2, BOTH_SOBELS)], 8: [(sort_words, 3)], 9: [(turn_squares, 3), (lay_state, 3)], 10: [(quantise_perception, 3, STATE_ONLY), (quantise_perception, 3, BOTH_SOBELS)]}
         for k, (b, g) in enumerate(slots):
             for u in range(PAIR):

@@ -117,6 +117,7 @@ def tile_nn_kernel(tc, state_grid, w_hidden_words, w_hidden_scales, w_out_words,
         load_block(2)
         load_block(3)
         load_images(2, 1)
+        load_squares(2)
         load_planes(wo_planes, w_out_scales, slice(0, CHANNELS))
         nc.sync.dma_start(
             out=wo_words[:].bitcast(I32), in_=w_out_words.rearrange("g p n t -> p g (n t)").bitcast(I32)
@@ -397,8 +398,8 @@ def tile_nn_kernel(tc, state_grid, w_hidden_words, w_hidden_scales, w_out_words,
 
         slots = [(0, 0), (1, 0), (0, 1), (1, 1), (0, 2), (1, 2), (0, 3), (1, 3)]
         slots += [(b, g) for b in range(2, IMAGES) for g in range(HIDDEN_PASSES)]
-        tensor_extras = {(5,0): [(state_window, 2, 0), (state_window, 2, 1), (state_window, 2, 2), (state_out, 2, True)], (5,1): [(sobel_window, 2, 0), (sobel_out, 2, 0, True), (sobel_window, 2, 1), (sobel_out, 2, 1, False), (sobel_window, 2, 2), (sobel_out, 2, 2, True)], (7,1): [(second_layer, 0, 0)], (8,0): [(second_layer, 0, 1)], (8,1): [(second_layer, 0, 2), (sobel_window, 3, 0), (sobel_out, 3, 0, True), (sobel_window, 3, 1), (sobel_out, 3, 1, False), (sobel_window, 3, 2), (sobel_out, 3, 2, True)], (9,0): [(second_layer, 0, 3), (store, 0, 0, True, nc.sync), (store, 0, 1, False, nc.sync)], (10,0): [(second_layer, 1, 0)], (10,1): [(second_layer, 1, 1)], (11,0): [(second_layer, 1, 2)], (11,1): [(second_layer, 1, 3), (store, 1, 0, True, nc.sync), (store, 1, 1, False, nc.sync)], (13,0): [(second_layer, 2, 0)], (13,1): [(second_layer, 2, 1)], (14,0): [(second_layer, 2, 2)], (14,1): [(second_layer, 2, 3), (store, 2, 0, True, nc.sync), (store, 2, 1, False, nc.sync)]}
-        vector_extras = {0: [(sort_hidden_units, 1)], 2: [(sort_hidden_units, 2)], 4: [(sort_hidden_units, 3)], 6: [(quantise_perception, 2, STATE_ONLY), (quantise_perception, 2, BOTH_SOBELS)], 8: [(sort_words, 3)], 9: [(turn_squares, 3), (lay_state, 3)], 10: [(quantise_perception, 3, STATE_ONLY), (quantise_perception, 3, BOTH_SOBELS)]}
+        tensor_extras = {(5,1): [(sobel_window, 2, 0), (sobel_out, 2, 0, True), (sobel_window, 2, 1), (sobel_out, 2, 1, False), (sobel_window, 2, 2), (sobel_out, 2, 2, True)], (7,1): [(second_layer, 0, 0)], (8,0): [(second_layer, 0, 1)], (8,1): [(second_layer, 0, 2), (sobel_window, 3, 0), (sobel_out, 3, 0, True), (sobel_window, 3, 1), (sobel_out, 3, 1, False), (sobel_window, 3, 2), (sobel_out, 3, 2, True)], (9,0): [(second_layer, 0, 3), (store, 0, 0, True, nc.sync), (store, 0, 1, False, nc.sync)], (10,0): [(second_layer, 1, 0)], (10,1): [(second_layer, 1, 1)], (11,0): [(second_layer, 1, 2)], (11,1): [(second_layer, 1, 3), (store, 1, 0, True, nc.sync), (store, 1, 1, False, nc.sync)], (13,0): [(second_layer, 2, 0)], (13,1): [(second_layer, 2, 1)], (14,0): [(second_layer, 2, 2)], (14,1): [(second_layer, 2, 3), (store, 2, 0, True, nc.sync), (store, 2, 1, False, nc.sync)]}
+        vector_extras = {0: [(sort_hidden_units, 1)], 2: [(sort_hidden_units, 2)], 4: [(sort_hidden_units, 3)], 5: [(sort_words, 2), (turn_squares, 2)], 6: [(lay_state, 2), (quantise_perception, 2, BOTH_SOBELS), (quantise_perception, 2, STATE_ONLY)], 8: [(sort_words, 3)], 9: [(turn_squares, 3), (lay_state, 3)], 10: [(quantise_perception, 3, STATE_ONLY), (quantise_perception, 3, BOTH_SOBELS)]}
         for k, (b, g) in enumerate(slots):
             for u in range(PAIR):
                 if k == 15:

@@ -135,9 +135,10 @@ def tile_nn_kernel(tc, state_grid, w_hidden_words, w_hidden_scales, w_out_words,
         def build_taps(name, identity, inner_rows):
             rows = inner_rows + 2
             padded = keep.tile([P, WINDOW_ROWS, PADDED], BF16, name="padded_" + name)
-            nc.vector.tensor_copy(out=padded[:, :, 1 : 1 + SIDE].rearrange("k (h a) c -> k h a c", h=2), in_=identity)
-            nc.vector.tensor_copy(out=padded[:, :, 0:1], in_=padded[:, :, SIDE : SIDE + 1])
-            nc.vector.tensor_copy(out=padded[:, :, SIDE + 1 :], in_=padded[:, :, 1:2])
+            halves = padded[:].rearrange("k (h a) c -> k h a c", h=2)
+            nc.vector.tensor_copy(out=halves[:, :, :, 1 : 1 + SIDE], in_=identity)
+            nc.vector.tensor_copy(out=halves[:, :, :, 0:1], in_=identity[:, :, :, SIDE - 1 :])
+            nc.vector.tensor_copy(out=halves[:, :, :, 1 + SIDE :], in_=identity[:, :, :, 0:1])
             taps = keep.tile([P, FILTERS, inner_rows, SIDE], BF16, name="taps_" + name)
             diff_x = keep.tile([P, rows, SIDE], BF16, name="diff_x_" + name)
             part_x = keep.tile([P, inner_rows, SIDE], BF16, name="part_x_" + name)
@@ -231,21 +232,17 @@ def tile_nn_kernel(tc, state_grid, w_hidden_words, w_hidden_scales, w_out_words,
                 nc.vector.tensor_copy(out=place, in_=bank)
 
         def state_window(b, w):
-            if w == 0:
-                state_banks[b] = banks.tile([P, PACK, IMAGE], BF16, name="state_bank%d" % b, tag="bank")
-            first, width = inner(w)
+            width = inner(w)[1]
+            bank = banks.tile([P, PACK, width], BF16, name="state_bank%d_%d" % (b, w), tag="bank")
+            state_banks[b, w] = bank
             for t in range(PACK):
-                nc.tensor.matmul(
-                    out=state_banks[b][:, t, first : first + width],
-                    lhsT=channels_of(b, w, t),
-                    rhs=taps[w][:, STATE],
-                    start=True,
-                    stop=True,
-                )
+                nc.tensor.matmul(out=bank[:, t], lhsT=channels_of(b, w, t), rhs=taps[w][:, STATE], start=True, stop=True)
 
-        def state_out(b, on_scalar):
-            for place, part in round_the_grid(0, IMAGE):
-                copy_out(perception[b][:, STATE, place], state_banks[b][:, :, part].rearrange("p t q -> p q t"), on_scalar)
+        def state_out(b, w, on_scalar):
+            for place, part in round_the_grid(*inner(w)):
+                copy_out(
+                    perception[b][:, STATE, place], state_banks[b, w][:, :, part].rearrange("p t q -> p q t"), on_scalar
+                )
 
         def sobel_window(b, w):
             first, width = inner(w)
@@ -372,23 +369,33 @@ def tile_nn_kernel(tc, state_grid, w_hidden_words, w_hidden_scales, w_out_words,
 
         STATE_ONLY = slice(STATE, FILTERS)
         BOTH_SOBELS = slice(0, SOBELS)
-        for w in range(WINDOWS):
-            state_window(0, w)
-            sobel_window(0, w)
+        state_window(0, 0)
+        sobel_window(0, 0)
+        state_window(0, 1)
+        sobel_window(0, 1)
+        state_window(0, 2)
+        sobel_window(0, 2)
+        state_out(0, 0, on_scalar=False)
         sobel_out(0, 0, on_scalar=True)
+        state_out(0, 1, on_scalar=False)
+        state_out(0, 2, on_scalar=True)
         sobel_out(0, 1, on_scalar=False)
-        state_out(0, on_scalar=True)
-        sobel_out(0, 2, on_scalar=False)
+        sobel_out(0, 2, on_scalar=True)
         sort_block(0, 2)
-        quantise_perception(0, BOTH_SOBELS)
         quantise_perception(0, STATE_ONLY)
-        for w in range(WINDOWS):
-            state_window(1, w)
-            sobel_window(1, w)
+        quantise_perception(0, BOTH_SOBELS)
+        state_window(1, 0)
+        sobel_window(1, 0)
+        state_window(1, 1)
+        sobel_window(1, 1)
+        state_window(1, 2)
+        sobel_window(1, 2)
         keep_busy(8)
+        state_out(1, 0, on_scalar=True)
         sobel_out(1, 0, on_scalar=True)
+        state_out(1, 1, on_scalar=True)
         sobel_out(1, 1, on_scalar=True)
-        state_out(1, on_scalar=True)
+        state_out(1, 2, on_scalar=True)
         sort_block(0, 0)
         sort_planes(0)
         sort_block(0, 1)
@@ -398,8 +405,8 @@ def tile_nn_kernel(tc, state_grid, w_hidden_words, w_hidden_scales, w_out_words,
 
         slots = [(0, 0), (1, 0), (0, 1), (1, 1), (0, 2), (1, 2), (0, 3), (1, 3)]
         slots += [(b, g) for b in range(2, IMAGES) for g in range(HIDDEN_PASSES)]
-        tensor_extras = {(5,1): [(sobel_window, 2, 0), (sobel_out, 2, 0, True), (sobel_window, 2, 1), (sobel_out, 2, 1, False), (sobel_window, 2, 2), (sobel_out, 2, 2, True)], (7,1): [(second_layer, 0, 0)], (8,0): [(second_layer, 0, 1)], (8,1): [(second_layer, 0, 2), (sobel_window, 3, 0), (sobel_out, 3, 0, True), (sobel_window, 3, 1), (sobel_out, 3, 1, False), (sobel_window, 3, 2), (sobel_out, 3, 2, True)], (9,0): [(second_layer, 0, 3), (store, 0, 0, True, nc.sync), (store, 0, 1, False, nc.sync)], (10,0): [(second_layer, 1, 0)], (10,1): [(second_layer, 1, 1)], (11,0): [(second_layer, 1, 2)], (11,1): [(second_layer, 1, 3), (store, 1, 0, True, nc.sync), (store, 1, 1, False, nc.sync)], (13,0): [(second_layer, 2, 0)], (13,1): [(second_layer, 2, 1)], (14,0): [(second_layer, 2, 2)], (14,1): [(second_layer, 2, 3), (store, 2, 0, True, nc.sync), (store, 2, 1, False, nc.sync)]}
-        vector_extras = {0: [(sort_hidden_units, 1)], 2: [(sort_hidden_units, 2)], 4: [(sort_hidden_units, 3)], 5: [(sort_words, 2), (turn_squares, 2)], 6: [(lay_state, 2), (quantise_perception, 2, BOTH_SOBELS), (quantise_perception, 2, STATE_ONLY)], 8: [(sort_words, 3)], 9: [(turn_squares, 3), (lay_state, 3)], 10: [(quantise_perception, 3, STATE_ONLY), (quantise_perception, 3, BOTH_SOBELS)]}
+        tensor_extras = {(5,1): [(sobel_window, 2, 0), (sobel_out, 2, 0, True), (sobel_window, 2, 1), (sobel_out, 2, 1, True), (sobel_window, 2, 2), (sobel_out, 2, 2, True)], (7,1): [(second_layer, 0, 0)], (8,0): [(second_layer, 0, 1)], (8,1): [(second_layer, 0, 2), (sobel_window, 3, 0), (sobel_out, 3, 0, True), (sobel_window, 3, 1), (sobel_out, 3, 1, False), (sobel_window, 3, 2), (sobel_out, 3, 2, True)], (9,0): [(second_layer, 0, 3), (store, 0, 0, True, nc.sync), (store, 0, 1, False, nc.sync)], (10,0): [(second_layer, 1, 0)], (10,1): [(second_layer, 1, 1)], (11,0): [(second_layer, 1, 2)], (11,1): [(second_layer, 1, 3), (store, 1, 0, True, nc.sync), (store, 1, 1, False, nc.sync)], (13,0): [(second_layer, 2, 0)], (13,1): [(second_layer, 2, 1)], (14,0): [(second_layer, 2, 2)], (14,1): [(second_layer, 2, 3), (store, 2, 0, True, nc.sync), (store, 2, 1, False, nc.sync)]}
+        vector_extras = {0: [(sort_hidden_units, 1)], 2: [(sort_hidden_units, 2)], 4: [(sort_hidden_units, 3)], 5: [(sort_words, 2), (turn_squares, 2), (lay_state, 2)], 6: [(quantise_perception, 2, STATE_ONLY), (quantise_perception, 2, BOTH_SOBELS)], 8: [(sort_words, 3)], 9: [(turn_squares, 3), (lay_state, 3)], 10: [(quantise_perception, 3, STATE_ONLY), (quantise_perception, 3, BOTH_SOBELS)]}
         for k, (b, g) in enumerate(slots):
             for u in range(PAIR):
                 if k == 15:

from contextlib import ExitStack

import concourse.mybir as mybir
from concourse.masks import make_identity

F32 = mybir.dt.float32
BF16 = mybir.dt.bfloat16
I32 = mybir.dt.int32
U32 = mybir.dt.uint32
U8 = mybir.dt.uint8
FP8X4 = mybir.dt.float8_e4m3fn_x4
ALU = mybir.AluOpType
RELU = mybir.ActivationFunctionType.Relu

P = 128
PACK = 4
K_PASS = P * PACK
BANK = 512

IMAGES, SIDE, CHANNELS, HIDDEN = 4, 16, 512, 2048
IMAGE = SIDE * SIDE
HALVES = IMAGE // P
WINDOW_ROWS = P // SIDE
INNER_ROWS = WINDOW_ROWS - 2
WINDOWS = 3
FILTERS = 3
SOBELS = 2
STATE = 2
PASS_ORDER = (2, 0, 1)
HIDDEN_PASSES = HIDDEN // K_PASS
PAIR = 2
LINE = 4
PADDED = SIDE + 2
SQUARE = 32
BLOCKS = IMAGE // SQUARE
QUARTER = CHANNELS // 4
WARM_UP = 14

FLOPS = 2 * IMAGES * IMAGE * (FILTERS * CHANNELS * HIDDEN + HIDDEN * CHANNELS)


def tile_nn_kernel(tc, state_grid, w_hidden_words, w_hidden_scales, w_out_words, w_out_scales, out):
    nc = tc.nc
    state_rows = state_grid.rearrange("b h w c -> (b h w) c")
    out_rows = out.rearrange("b h w c -> (b h w) c")

    with ExitStack() as stack:
        stack.enter_context(tc.manual_schedule())
        keep = stack.enter_context(tc.tile_pool(name="keep", bufs=1))
        work = stack.enter_context(tc.tile_pool(name="work", bufs=2))
        banks = stack.enter_context(tc.psum_pool(name="banks", bufs=6))
        sums = stack.enter_context(tc.psum_pool(name="sums", bufs=2))

        ident_bf16 = keep.tile([P, P], BF16)
        make_identity(nc, ident_bf16[:])

        wh_planes_raw = keep.tile([P, HIDDEN], U8, align_bytes=64)
        wo_planes = keep.tile([P, CHANNELS], U8, align_bytes=64)
        nothing = keep.tile([P, P], BF16)
        nc.vector.memset(nothing[:], 0.0)
        nc.vector.memset(wh_planes_raw[:].bitcast(I32), 0)
        nc.vector.memset(wo_planes[:].bitcast(I32), 0)

        state = {}

        def load_images(first_image, together):
            raw = [
                keep.tile([P, together, CHANNELS], BF16, name="state%d_%d" % (first_image, w)) for w in range(WINDOWS)
            ]
            rows = state_rows[first_image * IMAGE : (first_image + together) * IMAGE, :].rearrange(
                "(b q) c -> q b c", b=together
            )
            for w in range(WINDOWS - 1):
                first = INNER_ROWS * w * SIDE
                nc.sync.dma_start(out=raw[w][:], in_=rows[first : first + P])
            nc.sync.dma_start(out=raw[-1][0::2], in_=rows[IMAGE - P // 2 :])
            nc.sync.dma_start(out=raw[-1][1::2], in_=rows[: P // 2])
            for b in range(together):
                state[first_image + b] = [window[:, b] for window in raw]

        def load_planes(planes, scales, columns):
            for quadrant in range(4):
                nc.sync.dma_start(
                    out=planes[32 * quadrant : 32 * quadrant + 4 * scales.shape[0], columns].bitcast(I32),
                    in_=scales[:, 4 * quadrant : 4 * quadrant + 4, columns].bitcast(I32),
                )

        wh_bytes = w_hidden_words.rearrange("f p n t -> p f (n t)")
        wh_raw = []

        def load_block(g):
            block = keep.tile([P, FILTERS, BANK], U32, name="wh_raw%d" % g, align_bytes=64)
            for filters in (slice(STATE, FILTERS), slice(0, SOBELS)) if g == 0 else (slice(0, FILTERS),):
                nc.sync.dma_start(
                    out=block[:, filters].bitcast(I32),
                    in_=wh_bytes[:, filters, g * BANK * PACK : (g + 1) * BANK * PACK].bitcast(I32),
                )
            wh_raw.append(block)

        square_raw = {}

        def load_squares(b):
            square_raw[b] = keep.tile([P, BLOCKS, QUARTER], BF16, name="square_raw%d" % b, align_bytes=64)
            rows = state_rows[b * IMAGE : (b + 1) * IMAGE, :]
            for quadrant in range(4):
                nc.sync.dma_start(
                    out=square_raw[b][SQUARE * quadrant : SQUARE * (quadrant + 1)],
                    in_=rows[:, quadrant * QUARTER : (quadrant + 1) * QUARTER].rearrange("(k p) c -> p k c", p=SQUARE),
                )

        wo_words = keep.tile([P, HIDDEN_PASSES, CHANNELS], U32, align_bytes=64)
        load_images(0, 2)
        load_block(0)
        load_planes(wh_planes_raw, w_hidden_scales, slice(0, BANK))
        load_block(1)
        load_planes(wh_planes_raw, w_hidden_scales, slice(BANK, HIDDEN))
        load_block(2)
        load_block(3)
        load_images(2, 1)
        load_squares(2)
        load_planes(wo_planes, w_out_scales, slice(0, CHANNELS))
        nc.sync.dma_start(
            out=wo_words[:].bitcast(I32), in_=w_out_words.rearrange("g p n t -> p g (n t)").bitcast(I32)
        )
        load_images(3, 1)
        load_squares(3)

        def keep_busy(passes):
            idle = sums.tile([P, P], F32, name="idle%d" % passes, tag="sums")
            for n in range(passes):
                nc.tensor.matmul(out=idle[:], lhsT=nothing[:], rhs=nothing[:], start=True, stop=True)

        keep_busy(WARM_UP)

        def build_taps(name, identity, inner_rows):
            rows = inner_rows + 2
            padded = keep.tile([P, WINDOW_ROWS, PADDED], BF16, name="padded_" + name)
            halves = padded[:].rearrange("k (h a) c -> k h a c", h=2)
            nc.vector.tensor_copy(out=halves[:, :, :, 1 : 1 + SIDE], in_=identity)
            nc.vector.tensor_copy(out=halves[:, :, :, 0:1], in_=identity[:, :, :, SIDE - 1 :])
            nc.vector.tensor_copy(out=halves[:, :, :, 1 + SIDE :], in_=identity[:, :, :, 0:1])
            taps = keep.tile([P, FILTERS, inner_rows, SIDE], BF16, name="taps_" + name)
            diff_x = keep.tile([P, rows, SIDE], BF16, name="diff_x_" + name)
            part_x = keep.tile([P, inner_rows, SIDE], BF16, name="part_x_" + name)
            part_y = keep.tile([P, rows, SIDE], BF16, name="part_y_" + name)
            sum_y = keep.tile([P, rows, SIDE], BF16, name="sum_y_" + name)
            left, centre, right = (padded[:, :rows, j : j + SIDE] for j in range(3))
            nc.vector.tensor_sub(out=diff_x[:], in0=right, in1=left)
            nc.vector.tensor_copy(out=taps[:, STATE], in_=centre[:, 1 : 1 + inner_rows, :])
            nc.vector.scalar_tensor_tensor(out=part_y[:], in0=centre, scalar=2.0, in1=left, op0=ALU.mult, op1=ALU.add)
            nc.vector.scalar_tensor_tensor(
                out=part_x[:],
                in0=diff_x[:, 1 : 1 + inner_rows, :],
                scalar=2.0,
                in1=diff_x[:, :inner_rows, :],
                op0=ALU.mult,
                op1=ALU.add,
            )
            nc.vector.tensor_add(out=sum_y[:], in0=part_y[:], in1=right)
            nc.vector.tensor_add(out=taps[:, 0], in0=part_x[:], in1=diff_x[:, 2:, :])
            nc.vector.tensor_sub(out=taps[:, 1], in0=sum_y[:, 2:, :], in1=sum_y[:, :inner_rows, :])
            return taps[:].rearrange("k f o j -> k f (o j)")

        taps = [build_taps("plain", ident_bf16[:].rearrange("k (h a c) -> k h a c", h=2, c=SIDE), INNER_ROWS)] * 2
        taps.append(
            build_taps("woven", ident_bf16[:].rearrange("k (a c h) -> k h a c", h=2, c=SIDE), SIDE - 2 * INNER_ROWS)
        )

        wh_planes = keep.tile([P, HIDDEN], U8, align_bytes=64)
        wh_words = {}
        state_banks = {}
        sobel_banks = {}
        squares = {}
        out_sums = {}
        perception = [
            keep.tile([P, FILTERS, IMAGE, PACK], BF16, name="perception%d" % b, align_bytes=64) for b in range(IMAGES)
        ]
        perception_words = [
            keep.tile([P, FILTERS, IMAGE], U32, name="perception_words%d" % b, align_bytes=64) for b in range(IMAGES)
        ]
        perception_scales = [
            keep.tile([P, FILTERS, IMAGE], U8, name="perception_scales%d" % b, align_bytes=64) for b in range(IMAGES)
        ]
        hidden = [
            keep.tile([P, HIDDEN_PASSES, IMAGE, PACK], BF16, name="hidden%d" % b, align_bytes=64) for b in range(IMAGES)
        ]
        hidden_words = [
            keep.tile([P, HIDDEN_PASSES, IMAGE], U32, name="hidden_words%d" % b, align_bytes=64) for b in range(IMAGES)
        ]
        hidden_scales = [
            keep.tile([P, HIDDEN_PASSES, IMAGE], U8, name="hidden_scales%d" % b, align_bytes=64) for b in range(IMAGES)
        ]

        def sort_planes(g):
            columns = slice(g * BANK, (g + 1) * BANK)
            nc.vector.tensor_copy(
                out=wh_planes[:, columns].rearrange("r (t m) -> r t m", t=PACK),
                in_=wh_planes_raw[:, columns].rearrange("r (m t) -> r t m", t=PACK),
            )

        def sort_block(g, f, engine=None):
            if g not in wh_words:
                wh_words[g] = keep.tile([P, FILTERS, PACK, P], U32, name="wh_words%d" % g, align_bytes=64)
            (engine or nc.vector).tensor_copy(
                out=wh_words[g][:, f].bitcast(I32).rearrange("k t (c i) -> k c t i", i=LINE),
                in_=wh_raw[g][:, f, :].bitcast(I32).rearrange("k (c i t) -> k c t i", i=LINE, t=PACK),
            )

        def sort_hidden_units(g):
            for f in PASS_ORDER:
                sort_block(g, f)
            sort_planes(g)

        def inner(w):
            first = INNER_ROWS * w * SIDE
            return first, min(INNER_ROWS * SIDE, IMAGE - first)

        def round_the_grid(first, width):
            inside = min(width, IMAGE - SIDE - first)
            parts = [(slice(first + SIDE, first + SIDE + inside), slice(0, inside))]
            if inside < width:
                parts.append((slice(0, width - inside), slice(inside, width)))
            return parts

        def channels_of(b, w, t):
            return state[b][w].rearrange("q (p t) -> q t p", t=PACK)[:, t, :]

        def copy_out(place, bank, on_scalar):
            if on_scalar:
                nc.scalar.copy(out=place, in_=bank)
            else:
                nc.vector.tensor_copy(out=place, in_=bank)

        def state_window(b, w):
            width = inner(w)[1]
            bank = banks.tile([P, PACK, width], BF16, name="state_bank%d_%d" % (b, w), tag="bank")
            state_banks[b, w] = bank
            for t in range(PACK):
                nc.tensor.matmul(out=bank[:, t], lhsT=channels_of(b, w, t), rhs=taps[w][:, STATE], start=True, stop=True)

        def state_out(b, w, on_scalar):
            for place, part in round_the_grid(*inner(w)):
                copy_out(
                    perception[b][:, STATE, place], state_banks[b, w][:, :, part].rearrange("p t q -> p q t"), on_scalar
                )

        def sobel_window(b, w):
            first, width = inner(w)
            bank = banks.tile([P, PACK, SOBELS, width], BF16, name="sobel_bank%d_%d" % (b, w), tag="bank")
            sobel_banks[b, w] = bank
            for t in range(PACK):
                nc.tensor.matmul(
                    out=bank[:, t], lhsT=channels_of(b, w, t), rhs=taps[w][:, :SOBELS], start=True, stop=True
                )

        def sobel_out(b, w, on_scalar):
            first, width = inner(w)
            for place, part in round_the_grid(first, width):
                copy_out(
                    perception[b][:, :SOBELS, place, :], sobel_banks[b, w][:, :, :, part].rearrange("p t f q -> p f q t"), on_scalar
                )

        def sort_words(b):
            squares[b] = work.tile([P, BLOCKS, 2, SQUARE], I32, name="by_word%d" % b, tag="by_word", align_bytes=64)
            nc.vector.tensor_copy(
                out=squares[b][:],
                in_=square_raw[b][:].bitcast(I32).rearrange("p k (r v) -> p k v r", v=2),
            )

        def turn_squares(b):
            turned = work.tile([P, BLOCKS, 2, SQUARE], I32, name="turned%d" % b, tag="turned", align_bytes=64)
            nc.vector.transpose(
                out=turned[:].rearrange("p k v q -> p (k v q)").bitcast(F32),
                in_=squares[b][:].rearrange("p k v q -> p (k v q)").bitcast(F32),
            )
            squares[b] = turned

        def lay_state(b):
            nc.vector.tensor_copy(
                out=perception[b][:, STATE].rearrange("p q t -> p (q t)").bitcast(I32).rearrange(
                    "p (k q v) -> p k q v", k=BLOCKS, v=2
                ),
                in_=squares[b][:].rearrange("p k v q -> p k q v"),
            )

        def quantise_perception(b, filters):
            nc.vector.quantize_mx(
                out=perception_words[b][:, filters, :].rearrange("p f q -> p (f q)").bitcast(FP8X4),
                scales=perception_scales[b][:, filters, :].rearrange("p f q -> p (f q)"),
                in_=perception[b][:, filters].rearrange("p f q t -> p (f q t)"),
            )

        def relu_out(place, bank, on_scalar):
            if on_scalar:
                nc.scalar.activation(out=place, in_=bank, func=RELU)
            else:
                nc.vector.tensor_scalar_max(out=place, in0=bank, scalar1=0.0)

        def first_layer(b, g, u, on_scalar, split=False):
            bank = banks.tile([P, PAIR, IMAGE], F32, tag="bank")
            for e in range(PAIR):
                t = PAIR * u + e
                first = (g * PACK + t) * P
                for f in PASS_ORDER:
                    nc.tensor.matmul_mx(
                        out=bank[:, e, :],
                        lhsT=wh_words[g][:, f, t, :].bitcast(FP8X4),
                        lhsT_scale=wh_planes[4 * f : P, first : first + P],
                        rhs=perception_words[b][:, f, :].bitcast(FP8X4),
                        rhs_scale=perception_scales[b][:, f, :],
                        start=(f == PASS_ORDER[0]),
                        stop=(f == PASS_ORDER[-1]),
                    )
            place = hidden[b][:, g, :, PAIR * u : PAIR * (u + 1)]
            side_by_side = bank[:].rearrange("p e q -> p q e")
            if split:
                for half in range(HALVES):
                    pixels = slice(half * P, (half + 1) * P)
                    relu_out(place[:, pixels], side_by_side[:, pixels], half == 0)
            else:
                relu_out(place, side_by_side, on_scalar)

        def first_layer_tile(b, g, half, on_scalar):
            pixels = slice(half * P, (half + 1) * P)
            bank = banks.tile([P, PACK, P], F32, tag="bank")
            for t in range(PACK):
                first = (g * PACK + t) * P
                for f in PASS_ORDER:
                    nc.tensor.matmul_mx(
                        out=bank[:, t, :],
                        lhsT=wh_words[g][:, f, t, :].bitcast(FP8X4),
                        lhsT_scale=wh_planes[4 * f : P, first : first + P],
                        rhs=perception_words[b][:, f, pixels].bitcast(FP8X4),
                        rhs_scale=perception_scales[b][:, f, pixels],
                        start=(f == PASS_ORDER[0]),
                        stop=(f == PASS_ORDER[-1]),
                    )
            relu_out(hidden[b][:, g, pixels, :], bank[:].rearrange("p t q -> p q t"), on_scalar)

        def quantise_hidden(b, g, pixels=slice(0, IMAGE)):
            nc.vector.quantize_mx(
                out=hidden_words[b][:, g, pixels].bitcast(FP8X4),
                scales=hidden_scales[b][:, g, pixels],
                in_=hidden[b][:, g, pixels].rearrange("p q t -> p (q t)"),
            )

        def second_layer(b, g, halves=range(HALVES), columns=slice(0, CHANNELS)):
            for half in halves:
                key = (b, half, columns.start)
                if g == 0:
                    pool, tag = (banks, "bank") if b == IMAGES - 1 else (sums, "sums")
                    out_sums[key] = pool.tile([P, columns.stop - columns.start], F32, name="sums%d_%d_%d" % key, tag=tag)
                nc.tensor.matmul_mx(
                    out=out_sums[key][:],
                    lhsT=hidden_words[b][:, g, half * P : (half + 1) * P].bitcast(FP8X4),
                    lhsT_scale=hidden_scales[b][:, g, half * P : (half + 1) * P],
                    rhs=wo_words[:, g, columns].bitcast(FP8X4),
                    rhs_scale=wo_planes[4 * g : P, columns],
                    start=(g == 0),
                    stop=(g == HIDDEN_PASSES - 1),
                )

        def store(b, half, on_scalar, queue, columns=slice(0, CHANNELS)):
            key = (b, half, columns.start)
            result = work.tile([P, columns.stop - columns.start], F32, name="result%d_%d_%d" % key, tag="result", bufs=2 * IMAGES + 2)
            copy_out(result[:], out_sums[key][:], on_scalar)
            first = b * IMAGE + half * P
            queue.dma_start(out=out_rows[first : first + P, columns], in_=result[:])

        STATE_ONLY = slice(STATE, FILTERS)
        BOTH_SOBELS = slice(0, SOBELS)
        state_window(0, 0)
        sobel_window(0, 0)
        state_window(0, 1)
        sobel_window(0, 1)
        state_window(0, 2)
        sobel_window(0, 2)
        state_out(0, 0, on_scalar=False)
        sobel_out(0, 0, on_scalar=True)
        state_out(0, 1, on_scalar=False)
        state_out(0, 2, on_scalar=True)
        sobel_out(0, 1, on_scalar=False)
        sobel_out(0, 2, on_scalar=True)
        sort_block(0, 2)
        quantise_perception(0, STATE_ONLY)
        quantise_perception(0, BOTH_SOBELS)
        state_window(1, 0)
        sobel_window(1, 0)
        state_window(1, 1)
        sobel_window(1, 1)
        state_window(1, 2)
        sobel_window(1, 2)
        keep_busy(8)
        state_out(1, 0, on_scalar=True)
        sobel_out(1, 0, on_scalar=True)
        state_out(1, 1, on_scalar=True)
        sobel_out(1, 1, on_scalar=True)
        state_out(1, 2, on_scalar=True)
        sort_block(0, 0)
        sort_planes(0)
        sort_block(0, 1)
        sobel_out(1, 2, on_scalar=False)
        quantise_perception(1, BOTH_SOBELS)
        quantise_perception(1, STATE_ONLY)

        slots = [(0, 0), (1, 0), (0, 1), (1, 1), (0, 2), (1, 2), (0, 3), (1, 3)]
        slots += [(b, g) for b in range(2, IMAGES) for g in range(HIDDEN_PASSES)]
        tensor_extras = {(5,1): [(sobel_window, 2, 0), (sobel_out, 2, 0, True), (sobel_window, 2, 1), (sobel_out, 2, 1, True), (sobel_window, 2, 2), (sobel_out, 2, 2, True)], (7,1): [(second_layer, 0, 0)], (8,0): [(second_layer, 0, 1)], (8,1): [(second_layer, 0, 2), (sobel_window, 3, 0), (sobel_out, 3, 0, True), (sobel_window, 3, 1), (sobel_out, 3, 1, False), (sobel_window, 3, 2), (sobel_out, 3, 2, True)], (9,0): [(second_layer, 0, 3), (store, 0, 0, True, nc.sync), (store, 0, 1, False, nc.sync)], (10,0): [(second_layer, 1, 0)], (10,1): [(second_layer, 1, 1)], (11,0): [(second_layer, 1, 2)], (11,1): [(second_layer, 1, 3), (store, 1, 0, True, nc.sync), (store, 1, 1, False, nc.sync)], (13,0): [(second_layer, 2, 0)], (13,1): [(second_layer, 2, 1)], (14,0): [(second_layer, 2, 2)], (14,1): [(second_layer, 2, 3), (store, 2, 0, True, nc.sync), (store, 2, 1, False, nc.sync)]}
        vector_extras = {0: [(sort_hidden_units, 1)], 2: [(sort_hidden_units, 2)], 4: [(sort_hidden_units, 3)], 5: [(sort_words, 2), (turn_squares, 2), (lay_state, 2)], 6: [(quantise_perception, 2, STATE_ONLY), (quantise_perception, 2, BOTH_SOBELS)], 8: [(sort_words, 3)], 9: [(turn_squares, 3), (lay_state, 3)], 10: [(quantise_perception, 3, STATE_ONLY), (quantise_perception, 3, BOTH_SOBELS)]}
        for k, (b, g) in enumerate(slots):
            for u in range(PAIR):
                if k == 15:
                    first_layer_tile(b, g, u, on_scalar=True)
                else:
                    first_layer(b, g, u, on_scalar=(u == 1 or k in (0, 2, 4)))
                if u == 0 and k > 0:
                    quantise_hidden(*slots[k - 1])
                if u == 0 and k == 15:
                    quantise_hidden(b, g, slice(0, P))
                for call, *args in tensor_extras.get((k, u), ()):
                    call(*args)
            for call, *args in vector_extras.get(k, ()):
                call(*args)
        quantise_hidden(3, 3, slice(P, IMAGE))
        left, right = slice(0, CHANNELS // 2), slice(CHANNELS // 2, CHANNELS)
        for g in range(HIDDEN_PASSES):
            second_layer(3, g, (0,))
        store(3, 0, on_scalar=True, queue=nc.scalar)
        for g in range(HIDDEN_PASSES):
            second_layer(3, g, (1,), left)
        store(3, 1, on_scalar=False, queue=nc.sync, columns=left)
        for g in range(HIDDEN_PASSES):
            second_layer(3, g, (1,), right)
        store(3, 1, on_scalar=False, queue=nc.sync, columns=right)
